import numpy as np
import ml_dtypes


def mxq(x, axis, fmt="e4m3"):
    dtype, down = {"e4m3": (ml_dtypes.float8_e4m3fn, 7), "e5m2": (ml_dtypes.float8_e5m2, 14)}[fmt]
    v = np.moveaxis(np.asarray(x, np.float32).astype(ml_dtypes.bfloat16).astype(np.float64), axis, -1)
    blocks = v.reshape(v.shape[:-1] + (-1, 32))
    amax = np.abs(blocks).max(-1, keepdims=True)
    byte = np.maximum(np.where(amax > 0, np.frexp(amax)[1] - 1 + 127, 0) - down, 1)
    scale = np.exp2(byte - 127.0)
    codes = (blocks / scale).astype(np.float32).astype(dtype).astype(np.float64)
    return np.moveaxis((codes * scale).reshape(v.shape), -1, axis)


WIDE = False


def mx_kscale(k):
    if not WIDE:
        return np.ones(k)
    levels = np.array([10, -10, 5, -5, 0])
    if k % 512:
        return np.exp2(np.random.permutation(np.resize(levels, k // 32))).repeat(32)
    a = np.empty((k // 512, 16))
    for p in range(k // 512):
        a[p, :8] = np.random.permutation(np.resize(levels, 8))
        for g in range(8):
            far = levels[np.abs(levels - a[p, g]) >= 10]
            a[p, g + 8] = far[np.random.randint(len(far))]
    return np.exp2(a.ravel()).repeat(32)


BF16 = ml_dtypes.bfloat16


def bf(x):
    return np.asarray(x, np.float32).astype(BF16)


def f64(x):
    return np.asarray(x).astype(np.float64)


L, P, B, H = 4, 1, 2048, 1024
KEEP_PROB = 0.7


def preact(h_in, w, masks, mu, sigma, z):
    wm = f64(w)[0] * f64(masks)[0]
    noise = np.exp(f64(mu)[0][None, :] + f64(sigma)[0][None, :] * f64(z)[0])
    return f64(h_in) @ wm.T + noise


def setup_inputs():
    s = mx_kscale(B)[:, None]
    u = mx_kscale(H)
    w0 = bf(np.random.standard_normal((P, H, H)) / np.sqrt(H))
    h0 = bf(np.random.standard_normal((B, H)) * 1.3)
    masks = bf(np.random.uniform(size=(P, H, H)) < KEEP_PROB)
    mu = bf(np.random.uniform(-0.5, 0.5, (P, H)))
    sigma = bf(np.random.uniform(0.05, 0.5, (P, H)))
    z = bf(np.random.standard_normal((P, B, H)))
    g = np.random.standard_normal((B, H)) * np.exp2(np.random.randint(-6, 1, (B, 1))) * 2.0
    pre = preact(h0, w0, masks, mu, sigma, z)
    return {"h_in": bf(f64(h0) * s),
            "w": bf(f64(w0) / u[None, :, None]),
            "masks": masks,
            "mu": mu,
            "sigma": sigma,
            "z": z,
            "pre": np.asarray(pre, np.float32),
            "grad_out": bf(g / s * u[None, :])}


def reference(h_in, w, masks, mu, sigma, z, pre, grad_out):
    m = f64(masks)[0]
    wm = f64(w)[0] * m
    dz = np.where(f64(pre) > 0.0, f64(grad_out), 0.0)
    dh = mxq(dz, 1, "e5m2") @ mxq(wm, 0, "e4m3")
    dwm = mxq(dz, 0, "e5m2").T @ mxq(f64(h_in), 0, "e4m3")
    dw = (dwm * m)[None, :, :]
    return dh, dw

@@ -1,0 +1,377 @@
+from contextlib import ExitStack
+
+import concourse.mybir as mybir
+from concourse.masks import make_identity
+
+TOKENS, FEATS, INS = 2048, 1024, 1024
+FLOPS = 2 * (2 * TOKENS * FEATS * INS)
+BYTES = 2 * (TOKENS * INS + 2 * FEATS * INS + TOKENS * FEATS) + 4 * (TOKENS * FEATS + TOKENS * INS + FEATS * INS)
+
+F32 = mybir.dt.float32
+BF16 = mybir.dt.bfloat16
+U32 = mybir.dt.uint32
+U8 = mybir.dt.uint8
+E4M3 = mybir.dt.float8_e4m3fn_x4
+E5M2 = mybir.dt.float8_e5m2_x4
+MULT = mybir.AluOpType.mult
+IS_GT = mybir.AluOpType.is_gt
+
+P = 128
+PACK = 4
+HALF = P * PACK
+GROUPS = TOKENS // HALF
+
+IN_TURN_BANKS = ((1, 1), (1, 2))
+
+
+def tile_scm_mlp_pa_v_kernel(tc, h_in, w, masks, mu, sigma, z, pre, grad_out, out_0, out_1):
+    nc = tc.nc
+    pre_v = pre.rearrange("(g p j) w -> g p j w", p=P, j=PACK)
+    grad_v = grad_out.rearrange("(g p j) w -> g p j w", p=P, j=PACK)
+    h_v = h_in.rearrange("(g p j) i -> g p j i", p=P, j=PACK)
+    w_v = w[0, :, :].rearrange("(f q t) i -> f q t i", q=P, t=PACK)
+    mask_v = masks[0, :, :].rearrange("(f q t) i -> f q t i", q=P, t=PACK)
+    dx_v = out_0.rearrange("(g p j) i -> g p j i", p=P, j=PACK)
+    dw_v = out_1[0, :, :].rearrange("(f q t) i -> f q t i", q=P, t=PACK)
+
+    def half(n):
+        return slice(n * HALF, (n + 1) * HALF)
+
+    with ExitStack() as ctx:
+        keep = ctx.enter_context(tc.tile_pool(name="keep", bufs=1))
+        pool = ctx.enter_context(tc.tile_pool(name="pool", bufs=2))
+        psum = ctx.enter_context(tc.psum_pool(name="psum", bufs=2))
+
+        ident = keep.tile([P, P], F32, name="ident")
+        make_identity(nc, ident[:])
+
+        z_tok_codes = keep.tile([P, GROUPS, FEATS], U32, align_bytes=64, name="z_tok_codes")
+        z_tok_scales = keep.tile([P, GROUPS, FEATS], U8, align_bytes=64, name="z_tok_scales")
+        h_codes = keep.tile([P, GROUPS, INS], U32, align_bytes=64, name="h_codes")
+        h_scales = keep.tile([P, GROUPS, INS], U8, align_bytes=64, name="h_scales")
+        w_codes = keep.tile([P, 2, INS], U32, align_bytes=64, name="w_codes")
+        w_scales = keep.tile([P, 2, INS], U8, align_bytes=64, name="w_scales")
+        mask = keep.tile([P, 2, PACK, INS], BF16, align_bytes=64, name="mask")
+
+        pre_t, grad_t, h_t, w_t, dz_t = {}, {}, {}, {}, {}
+        dz_tok_by4, dz_feat_by4, h_by4, w_by4 = {}, {}, {}, {}
+        z_feat_codes, z_feat_scales = {}, {}
+        dx_t, dw_acc = {}, {}
+
+        def move(engine, out, in_):
+            if engine == "s":
+                nc.scalar.copy(out=out, in_=in_)
+            else:
+                nc.vector.tensor_copy(out=out, in_=in_)
+
+        def load_step_part(src, tiles, dtype, tag, g, cols, rows):
+            if g not in tiles:
+                new = pool.tile([P, PACK, FEATS], dtype, tag=tag, name="group_tile")
+                tiles[g] = new
+            nc.sync.dma_start(out=tiles[g][:, rows, cols], in_=src[g, :, rows, cols])
+
+        def load_pre(g, cols=slice(0, FEATS), rows=slice(0, PACK)):
+            load_step_part(pre_v, pre_t, F32, "pre", g, cols, rows)
+
+        def load_grad(g, cols=slice(0, FEATS), rows=slice(0, PACK)):
+            load_step_part(grad_v, grad_t, BF16, "grad", g, cols, rows)
+
+        def load_h(g):
+            new = pool.tile([P, PACK, INS], BF16, tag="h_or_w", bufs=3, name="h_tile")
+            nc.sync.dma_start(out=new[:], in_=h_v[g, :, :, :])
+            h_t[g] = new
+
+        def load_w(f):
+            new = pool.tile([P, PACK, INS], BF16, tag="h_or_w", bufs=3, name="w_tile")
+            nc.sync.dma_start(out=new[:], in_=w_v[f, :, :, :])
+            w_t[f] = new
+
+        def load_mask(f):
+            nc.sync.dma_start(out=mask[:, f, :, :], in_=mask_v[f, :, :, :])
+
+        def gate(g, f, rows=slice(0, PACK)):
+            if (g, f) not in dz_t:
+                new = pool.tile([P, PACK, HALF], BF16, tag="dz", bufs=5, align_bytes=64, name="dz_tile")
+                dz_t[g, f] = new
+            nc.vector.scalar_tensor_tensor(
+                out=dz_t[g, f][:, rows, :],
+                in0=pre_t[g][:, rows, half(f)],
+                scalar=0.0,
+                in1=grad_t[g][:, rows, half(f)],
+                op0=IS_GT,
+                op1=MULT,
+            )
+
+        def turn(g, f):
+            words = dz_t[g, f][:].rearrange("p j w -> p (j w)").bitcast(F32)
+            new = pool.tile([P, PACK, P, PACK], BF16, tag="dz_feat_by4", align_bytes=64, name="feat_tile")
+            dz_feat_by4[g, f] = new
+            new_words = new[:].rearrange("q j p t -> q (j p t)").bitcast(F32)
+            new_words = new_words.rearrange("q (j p u) -> q j p u", j=PACK, u=2)
+            for pair in range(2):
+                bank = psum.tile([P, 2, 2, P], F32, tag="turn", name="turn_bank")
+                for k in range(2):
+                    for u in range(2):
+                        first = (2 * pair + k) * (HALF // 2) + u
+                        nc.tensor.transpose(bank[:, k, u, :], words[:, first : first + HALF // 2 - 1 : 2], ident[:])
+                nc.scalar.copy(
+                    out=new_words[:, 2 * pair : 2 * pair + 2, :, :], in_=bank[:].rearrange("q k u p -> q k p u")
+                )
+
+        def quant_feat(g, f):
+            if g not in z_feat_codes:
+                codes = pool.tile([P, 2, HALF], U32, tag="z_feat_codes", align_bytes=64, name="feat_codes")
+                scales = pool.tile([P, 2, HALF], U8, tag="z_feat_scales", align_bytes=64, name="feat_scales")
+                z_feat_codes[g], z_feat_scales[g] = codes, scales
+            nc.vector.quantize_mx(
+                out=z_feat_codes[g][:, f, :].bitcast(E5M2),
+                scales=z_feat_scales[g][:, f, :],
+                in_=dz_feat_by4[g, f][:].rearrange("q j p t -> q (j p t)"),
+            )
+
+        def spread_dz(g, f):
+            new = pool.tile([P, PACK, P, PACK], BF16, tag="dz_tok_by4", align_bytes=64, name="tok_tile")
+            nc.vector.tensor_copy(
+                out=new[:].rearrange("p t q j -> p q t j"),
+                in_=dz_t[g, f][:].rearrange("p j (q t) -> p q t j", t=PACK),
+            )
+            dz_tok_by4[g, f] = new
+
+        def quant_tok(g, f):
+            nc.vector.quantize_mx(
+                out=z_tok_codes[:, g, half(f)].bitcast(E5M2),
+                scales=z_tok_scales[:, g, half(f)],
+                in_=dz_tok_by4[g, f][:].rearrange("p t q j -> p (t q j)"),
+            )
+
+        def by4(engine, src):
+            new = pool.tile([P, HALF, PACK], BF16, tag="by4", bufs=3, align_bytes=64, name="by4_tile")
+            move(engine, new[:].rearrange("p (c i) t -> p c t i", i=4), src.rearrange("p t (c i) -> p c t i", i=4))
+            return new
+
+        def spread_h(g, n, engine="s"):
+            h_by4[g, n] = by4(engine, h_t[g][:, :, half(n)])
+
+        def quant_h(g, n):
+            nc.vector.quantize_mx(
+                out=h_codes[:, g, half(n)].bitcast(E4M3),
+                scales=h_scales[:, g, half(n)],
+                in_=h_by4[g, n][:].rearrange("p i j -> p (i j)"),
+            )
+
+        def mask_w(f, n):
+            nc.vector.tensor_tensor(
+                out=w_t[f][:, :, half(n)], in0=w_t[f][:, :, half(n)], in1=mask[:, f, :, half(n)], op=MULT
+            )
+
+        def spread_w(f, n, engine="s"):
+            w_by4[f, n] = by4(engine, w_t[f][:, :, half(n)])
+
+        def quant_w(f, n):
+            nc.vector.quantize_mx(
+                out=w_codes[:, f, half(n)].bitcast(E4M3),
+                scales=w_scales[:, f, half(n)],
+                in_=w_by4[f, n][:].rearrange("q i t -> q (i t)"),
+            )
+
+        def dx(g, j, engines="ss"):
+            pair, k = divmod(j, 2)
+            if (g, pair) not in dx_t:
+                new = pool.tile([P, 2, INS], F32, tag="result", bufs=4, name="dx_tile")
+                dx_t[g, pair] = new
+            cols = slice(j * P, (j + 1) * P)
+            banks = []
+            for n in range(2):
+                bank = psum.tile([P, HALF], F32, tag="dx", name="dx_bank")
+                for f in range(2):
+                    nc.tensor.matmul_mx(
+                        out=bank[:],
+                        lhsT=z_feat_codes[g][:, f, cols].bitcast(E5M2),
+                        lhsT_scale=z_feat_scales[g][:, f, cols],
+                        rhs=w_codes[:, f, half(n)].bitcast(E4M3),
+                        rhs_scale=w_scales[:, f, half(n)],
+                        start=(f == 0),
+                        stop=(f == 1),
+                    )
+                banks.append(bank)
+            for n in range(2):
+                move(engines[n], dx_t[g, pair][:, k, half(n)], banks[n][:])
+
+        def store_dx(g, pair):
+            nc.sync.dma_start(out=dx_v[g, :, 2 * pair : 2 * pair + 2, :], in_=dx_t[g, pair][:])
+
+        def dw(f, t, *groups):
+            cols = slice(f * HALF + t * P, f * HALF + (t + 1) * P)
+            for g in groups:
+                for n in range(2):
+                    if g == 0:
+                        tag = "turn" if (f, t) in IN_TURN_BANKS else "dw" + str(n)
+                        bank = psum.tile([P, HALF], F32, tag=tag, name="dw_bank")
+                        dw_acc[f, t, n] = bank
+                    nc.tensor.matmul_mx(
+                        out=dw_acc[f, t, n][:],
+                        lhsT=z_tok_codes[:, g, cols].bitcast(E5M2),
+                        lhsT_scale=z_tok_scales[:, g, cols],
+                        rhs=h_codes[:, g, half(n)].bitcast(E4M3),
+                        rhs_scale=h_scales[:, g, half(n)],
+                        start=(g == 0),
+                        stop=(g == GROUPS - 1),
+                    )
+
+        def out_dw(f, t, stores=1):
+            new = pool.tile([P, INS], F32, tag="result", bufs=4, name="dw_tile")
+            for n in range(2):
+                nc.vector.tensor_tensor(
+                    out=new[:, half(n)], in0=dw_acc[f, t, n][:], in1=mask[:, f, t, half(n)], op=MULT
+                )
+                if stores == 2:
+                    nc.sync.dma_start(out=dw_v[f, :, t, half(n)], in_=new[:, half(n)])
+            if stores == 1:
+                nc.sync.dma_start(out=dw_v[f, :, t, :], in_=new[:])
+
+        with tc.manual_schedule():
+            load_w(0)
+            load_mask(0)
+            load_grad(0, cols=half(0), rows=slice(0, 2))
+            mask_w(0, 0)
+            load_pre(0, cols=half(0), rows=slice(0, 2))
+            mask_w(0, 1)
+            load_grad(0, cols=half(1))
+            spread_w(0, 0, "v")
+            load_pre(0, cols=half(1))
+            gate(0, 0, rows=slice(0, 2))
+            quant_w(0, 0)
+            load_pre(0, cols=half(0), rows=slice(2, 4))
+            load_grad(0, cols=half(0), rows=slice(2, 4))
+            spread_w(0, 1)
+            quant_w(0, 1)
+            load_h(0)
+            gate(0, 1)
+            load_w(1)
+            gate(0, 0, rows=slice(2, 4))
+            spread_dz(0, 1)
+            turn(0, 1)
+            spread_dz(0, 0)
+            spread_h(0, 0)
+            quant_tok(0, 0)
+            load_mask(1)
+            turn(0, 0)
+            quant_h(0, 0)
+            load_grad(1)
+            quant_feat(0, 0)
+            mask_w(1, 0)
+            spread_h(0, 1)
+            spread_w(1, 0)
+            mask_w(1, 1)
+            quant_feat(0, 1)
+            spread_w(1, 1, "v")
+            quant_w(1, 0)
+            quant_w(1, 1)
+            load_pre(1)
+            dx(0, 0)
+            quant_h(0, 1)
+            load_h(2)
+            quant_tok(0, 1)
+            gate(1, 0)
+            dx(0, 2)
+            gate(1, 1)
+            spread_h(2, 1, "v")
+            spread_h(2, 0)
+            spread_dz(1, 0)
+            load_h(1)
+            turn(1, 0)
+            load_grad(2)
+            dx(0, 3)
+            quant_feat(1, 0)
+            dw(0, 1, 0)
+            quant_h(2, 1)
+            turn(1, 1)
+            spread_h(1, 1)
+            dw(0, 0, 0)
+            quant_feat(1, 1)
+            dx(1, 2)
+            spread_h(1, 0)
+            quant_tok(1, 0)
+            quant_h(2, 0)
+            load_pre(2)
+            quant_h(1, 1)
+            gate(2, 0)
+            dx(1, 0)
+            gate(2, 1)
+            turn(2, 0)
+            dx(1, 1)
+            load_pre(3)
+            spread_dz(2, 0)
+            load_grad(3)
+            turn(2, 1)
+            quant_h(1, 0)
+            load_h(3)
+            dx(0, 1)
+            dw(0, 1, 1)
+            quant_feat(2, 0)
+            spread_h(3, 1)
+            quant_tok(2, 0)
+            store_dx(0, 1)
+            store_dx(0, 0)
+            dw(0, 0, 1)
+            dw(0, 1, 2)
+            dx(1, 3)
+            gate(3, 1)
+            turn(3, 1)
+            store_dx(1, 1)
+            quant_feat(2, 1)
+            dw(0, 0, 2)
+            gate(3, 0)
+            dx(2, 2)
+            spread_h(3, 0, "v")
+            spread_dz(3, 0)
+            turn(3, 0)
+            quant_h(3, 0)
+            dx(2, 3)
+            store_dx(1, 0)
+            store_dx(2, 1)
+            dw(1, 2, 0)
+            quant_tok(3, 0)
+            dx(2, 0)
+            quant_h(3, 1)
+            quant_feat(3, 1)
+            dw(0, 1, 3)
+            dx(2, 1)
+            out_dw(0, 1)
+            quant_feat(3, 0)
+            store_dx(2, 0)
+            dw(0, 0, 3)
+            dw(0, 2, 0)
+            spread_dz(1, 1)
+            spread_dz(2, 1)
+            quant_tok(1, 1)
+            out_dw(0, 0)
+            dx(3, 2)
+            dw(0, 2, 1, 2)
+            dx(3, 3)
+            dw(0, 2, 3)
+            out_dw(0, 2)
+            quant_tok(2, 1)
+            dx(3, 0)
+            dw(0, 3, 0)
+            spread_dz(3, 1)
+            dw(1, 2, 1)
+            dw(1, 0, 0)
+            store_dx(3, 1)
+            dw(1, 0, 1)
+            quant_tok(3, 1)
+            dw(1, 0, 2)
+            dx(3, 1, "vv")
+            dw(0, 3, 1)
+            dw(1, 2, 2, 3)
+            dw(0, 3, 2, 3)
+            store_dx(3, 0)
+            dw(1, 0, 3)
+            out_dw(1, 2)
+            dw(1, 1, 0, 1, 2, 3)
+            out_dw(0, 3)
+            out_dw(1, 0)
+            dw(1, 3, 0, 1)
+            out_dw(1, 1)
+            dw(1, 3, 2, 3)
+            out_dw(1, 3, stores=2)

@@ -20,43 +20,43 @@ P = 128
 PACK = 4
 HALF = P * PACK
 GROUPS = TOKENS // HALF
-
-IN_TURN_BANKS = ((1, 1), (1, 2))
+LAST = GROUPS - 1
+PAIR = 2 * FEATS
 
 
 def tile_scm_mlp_pa_v_kernel(tc, h_in, w, masks, mu, sigma, z, pre, grad_out, out_0, out_1):
     nc = tc.nc
-    pre_v = pre.rearrange("(g p j) w -> g p j w", p=P, j=PACK)
-    grad_v = grad_out.rearrange("(g p j) w -> g p j w", p=P, j=PACK)
-    h_v = h_in.rearrange("(g p j) i -> g p j i", p=P, j=PACK)
-    w_v = w[0, :, :].rearrange("(f q t) i -> f q t i", q=P, t=PACK)
-    mask_v = masks[0, :, :].rearrange("(f q t) i -> f q t i", q=P, t=PACK)
-    dx_v = out_0.rearrange("(g p j) i -> g p j i", p=P, j=PACK)
-    dw_v = out_1[0, :, :].rearrange("(f q t) i -> f q t i", q=P, t=PACK)
+    pre_v = pre.rearrange("(g p j) w -> g p (j w)", p=P, j=PACK)
+    grad_v = grad_out.rearrange("(g p j) w -> g p (j w)", p=P, j=PACK)
+    h_v = h_in.rearrange("(g p j) i -> g p (j i)", p=P, j=PACK)
+    w_v = w[0, :, :].rearrange("(f q t) i -> f q (t i)", q=P, t=PACK)
+    mask_v = masks[0, :, :].rearrange("(f q t) i -> f q (t i)", q=P, t=PACK)
+    dx_v = out_0.rearrange("(g p j) i -> g p (j i)", p=P, j=PACK)
+    dw_v = out_1[0, :, :].rearrange("(f q t) i -> f q (t i)", q=P, t=PACK)
 
-    def half(n):
-        return slice(n * HALF, (n + 1) * HALF)
+    def span(k, width):
+        return slice(k * width, (k + 1) * width)
 
     with ExitStack() as ctx:
         keep = ctx.enter_context(tc.tile_pool(name="keep", bufs=1))
         pool = ctx.enter_context(tc.tile_pool(name="pool", bufs=2))
-        psum = ctx.enter_context(tc.psum_pool(name="psum", bufs=2))
+        psum = ctx.enter_context(tc.psum_pool(name="psum", bufs=1))
 
         ident = keep.tile([P, P], F32, name="ident")
         make_identity(nc, ident[:])
 
-        z_tok_codes = keep.tile([P, GROUPS, FEATS], U32, align_bytes=64, name="z_tok_codes")
-        z_tok_scales = keep.tile([P, GROUPS, FEATS], U8, align_bytes=64, name="z_tok_scales")
-        h_codes = keep.tile([P, GROUPS, INS], U32, align_bytes=64, name="h_codes")
-        h_scales = keep.tile([P, GROUPS, INS], U8, align_bytes=64, name="h_scales")
-        w_codes = keep.tile([P, 2, INS], U32, align_bytes=64, name="w_codes")
-        w_scales = keep.tile([P, 2, INS], U8, align_bytes=64, name="w_scales")
-        mask = keep.tile([P, 2, PACK, INS], BF16, align_bytes=64, name="mask")
+        z_tok_codes = keep.tile([P, GROUPS * FEATS], U32, align_bytes=64, name="z_tok_codes")
+        z_tok_scales = keep.tile([P, GROUPS * FEATS], U8, align_bytes=64, name="z_tok_scales")
+        h_codes = keep.tile([P, GROUPS * INS], U32, align_bytes=64, name="h_codes")
+        h_scales = keep.tile([P, GROUPS * INS], U8, align_bytes=64, name="h_scales")
+        w_codes = keep.tile([P, 2 * INS], U32, align_bytes=64, name="w_codes")
+        w_scales = keep.tile([P, 2 * INS], U8, align_bytes=64, name="w_scales")
+        mask = keep.tile([P, 2 * PACK * INS], BF16, align_bytes=64, name="mask")
 
-        pre_t, grad_t, h_t, w_t, dz_t = {}, {}, {}, {}, {}
-        dz_tok_by4, dz_feat_by4, h_by4, w_by4 = {}, {}, {}, {}
-        z_feat_codes, z_feat_scales = {}, {}
-        dx_t, dw_acc = {}, {}
+        pre_t, dz_t, h_t, w_t = {}, {}, {}, {}
+        tok_by4, feat_by4, h_by4, w_by4 = {}, {}, {}, {}
+        feat_codes, feat_scales = {}, {}
+        turn_bank, dx_bank, dx_t, dw_bank, dw_t = {}, {}, {}, {}, {}
 
         def move(engine, out, in_):
             if engine == "s":
@@ -64,314 +64,272 @@ def tile_scm_mlp_pa_v_kernel(tc, h_in, w, masks, mu, sigma, z, pre, grad_out, ou
             else:
                 nc.vector.tensor_copy(out=out, in_=in_)
 
-        def load_step_part(src, tiles, dtype, tag, g, cols, rows):
-            if g not in tiles:
-                new = pool.tile([P, PACK, FEATS], dtype, tag=tag, name="group_tile")
-                tiles[g] = new
-            nc.sync.dma_start(out=tiles[g][:, rows, cols], in_=src[g, :, rows, cols])
+        def next_bank():
+            return psum.tile([P, HALF], F32, tag="bank", bufs=8, name="bank_tile")
 
-        def load_pre(g, cols=slice(0, FEATS), rows=slice(0, PACK)):
-            load_step_part(pre_v, pre_t, F32, "pre", g, cols, rows)
+        def load_pre(g, a):
+            new = keep.tile([P, PAIR], F32, tag="pre%d%d" % (g, a), name="pre_tile")
+            nc.sync.dma_start(out=new[:], in_=pre_v[g, :, span(a, PAIR)])
+            pre_t[g, a] = new
 
-        def load_grad(g, cols=slice(0, FEATS), rows=slice(0, PACK)):
-            load_step_part(grad_v, grad_t, BF16, "grad", g, cols, rows)
+        def load_grad(g, cols=slice(0, 2 * PAIR)):
+            if g not in dz_t:
+                new = keep.tile([P, 2 * PAIR], BF16, tag="dz%d" % g, align_bytes=64, name="dz_tile")
+                dz_t[g] = new
+            nc.sync.dma_start(out=dz_t[g][:, cols], in_=grad_v[g, :, cols])
 
         def load_h(g):
-            new = pool.tile([P, PACK, INS], BF16, tag="h_or_w", bufs=3, name="h_tile")
-            nc.sync.dma_start(out=new[:], in_=h_v[g, :, :, :])
+            new = pool.tile([P, PACK * INS], BF16, tag="rows", bufs=4, name="h_tile")
+            nc.sync.dma_start(out=new[:], in_=h_v[g, :, :])
             h_t[g] = new
 
         def load_w(f):
-            new = pool.tile([P, PACK, INS], BF16, tag="h_or_w", bufs=3, name="w_tile")
-            nc.sync.dma_start(out=new[:], in_=w_v[f, :, :, :])
+            new = pool.tile([P, PACK * INS], BF16, tag="rows", bufs=4, name="w_tile")
+            nc.sync.dma_start(out=new[:], in_=w_v[f, :, :])
+            nc.sync.dma_start(out=mask[:, span(f, PACK * INS)], in_=mask_v[f, :, :])
             w_t[f] = new
 
-        def load_mask(f):
-            nc.sync.dma_start(out=mask[:, f, :, :], in_=mask_v[f, :, :, :])
+        def gate(g, a):
+            rows = dz_t[g][:, span(a, PAIR)]
+            nc.vector.scalar_tensor_tensor(out=rows, in0=pre_t[g, a][:], scalar=0.0, in1=rows, op0=IS_GT, op1=MULT)
 
-        def gate(g, f, rows=slice(0, PACK)):
-            if (g, f) not in dz_t:
-                new = pool.tile([P, PACK, HALF], BF16, tag="dz", bufs=5, align_bytes=64, name="dz_tile")
-                dz_t[g, f] = new
-            nc.vector.scalar_tensor_tensor(
-                out=dz_t[g, f][:, rows, :],
-                in0=pre_t[g][:, rows, half(f)],
-                scalar=0.0,
-                in1=grad_t[g][:, rows, half(f)],
-                op0=IS_GT,
-                op1=MULT,
-            )
-
-        def turn(g, f):
-            words = dz_t[g, f][:].rearrange("p j w -> p (j w)").bitcast(F32)
-            new = pool.tile([P, PACK, P, PACK], BF16, tag="dz_feat_by4", align_bytes=64, name="feat_tile")
-            dz_feat_by4[g, f] = new
-            new_words = new[:].rearrange("q j p t -> q (j p t)").bitcast(F32)
-            new_words = new_words.rearrange("q (j p u) -> q j p u", j=PACK, u=2)
-            for pair in range(2):
-                bank = psum.tile([P, 2, 2, P], F32, tag="turn", name="turn_bank")
+        def turn(g, a):
+            words = dz_t[g][:].bitcast(F32)
+            for f in range(2):
+                new = next_bank()
                 for k in range(2):
                     for u in range(2):
-                        first = (2 * pair + k) * (HALF // 2) + u
-                        nc.tensor.transpose(bank[:, k, u, :], words[:, first : first + HALF // 2 - 1 : 2], ident[:])
-                nc.scalar.copy(
-                    out=new_words[:, 2 * pair : 2 * pair + 2, :, :], in_=bank[:].rearrange("q k u p -> q k p u")
+                        first = (2 * a + k) * (FEATS // 2) + f * (HALF // 2) + u
+                        nc.tensor.transpose(
+                            new[:, span(2 * k + u, P)], words[:, first : first + HALF // 2 - 1 : 2], ident[:]
+                        )
+                turn_bank[g, a, f] = new
+
+        def turn_out(g, a, engines="ss"):
+            new = pool.tile([P, PAIR], BF16, tag="feat_by4", align_bytes=64, name="feat_tile")
+            words = new[:].bitcast(F32)
+            for f in range(2):
+                move(
+                    engines[f],
+                    words[:, span(f, HALF)].rearrange("q (k p u) -> q k p u", k=2, u=2),
+                    turn_bank[g, a, f][:].rearrange("q (k u p) -> q k p u", k=2, u=2),
                 )
+            feat_by4[g, a] = new
 
-        def quant_feat(g, f):
-            if g not in z_feat_codes:
-                codes = pool.tile([P, 2, HALF], U32, tag="z_feat_codes", align_bytes=64, name="feat_codes")
-                scales = pool.tile([P, 2, HALF], U8, tag="z_feat_scales", align_bytes=64, name="feat_scales")
-                z_feat_codes[g], z_feat_scales[g] = codes, scales
-            nc.vector.quantize_mx(
-                out=z_feat_codes[g][:, f, :].bitcast(E5M2),
-                scales=z_feat_scales[g][:, f, :],
-                in_=dz_feat_by4[g, f][:].rearrange("q j p t -> q (j p t)"),
-            )
+        def quant_feat(g, a):
+            codes = pool.tile([P, HALF], U32, tag="feat_codes", bufs=3, align_bytes=64, name="feat_codes_tile")
+            scales = pool.tile([P, HALF], U8, tag="feat_scales", bufs=3, align_bytes=64, name="feat_scales_tile")
+            nc.vector.quantize_mx(out=codes[:].bitcast(E5M2), scales=scales[:], in_=feat_by4[g, a][:])
+            feat_codes[g, a], feat_scales[g, a] = codes, scales
 
-        def spread_dz(g, f):
-            new = pool.tile([P, PACK, P, PACK], BF16, tag="dz_tok_by4", align_bytes=64, name="tok_tile")
-            nc.vector.tensor_copy(
-                out=new[:].rearrange("p t q j -> p q t j"),
-                in_=dz_t[g, f][:].rearrange("p j (q t) -> p q t j", t=PACK),
-            )
-            dz_tok_by4[g, f] = new
+        def spread_dz(g, f, engine="v"):
+            new = pool.tile([P, PACK * HALF], BF16, tag="tok_by4", bufs=3, align_bytes=64, name="tok_tile")
+            src = dz_t[g][:].rearrange("p (j w) -> p j w", j=PACK)[:, :, span(f, HALF)]
+            if engine == "v":
+                nc.vector.tensor_copy(
+                    out=new[:].rearrange("p (t q j) -> p q t j", t=PACK, j=PACK),
+                    in_=src.rearrange("p j (q t) -> p q t j", t=PACK),
+                )
+            else:
+                nc.scalar.copy(
+                    out=new[:].rearrange("p (t c r j) -> p c t j r", t=PACK, r=2, j=PACK),
+                    in_=src.rearrange("p j (c r t) -> p c t j r", r=2, t=PACK),
+                )
+            tok_by4[g, f] = new
 
         def quant_tok(g, f):
+            cols = span(2 * g + f, HALF)
             nc.vector.quantize_mx(
-                out=z_tok_codes[:, g, half(f)].bitcast(E5M2),
-                scales=z_tok_scales[:, g, half(f)],
-                in_=dz_tok_by4[g, f][:].rearrange("p t q j -> p (t q j)"),
+                out=z_tok_codes[:, cols].bitcast(E5M2), scales=z_tok_scales[:, cols], in_=tok_by4[g, f][:]
             )
 
-        def by4(engine, src):
-            new = pool.tile([P, HALF, PACK], BF16, tag="by4", bufs=3, align_bytes=64, name="by4_tile")
-            move(engine, new[:].rearrange("p (c i) t -> p c t i", i=4), src.rearrange("p t (c i) -> p c t i", i=4))
-            return new
+        def by4(engine, tiles, key, rows, n, part, parts):
+            if part == 0:
+                new = pool.tile([P, PACK * HALF], BF16, tag="by4", bufs=3, align_bytes=64, name="by4_tile")
+                tiles[key] = new
+            width = HALF // parts
+            src = rows[:].rearrange("p (t i) -> p t i", t=PACK)[:, :, span(n * parts + part, width)]
+            move(
+                engine,
+                tiles[key][:, span(part, PACK * width)].rearrange("p (c i t) -> p c t i", i=4, t=PACK),
+                src.rearrange("p t (c i) -> p c t i", i=4),
+            )
 
-        def spread_h(g, n, engine="s"):
-            h_by4[g, n] = by4(engine, h_t[g][:, :, half(n)])
+        def spread_h(g, n, engine="s", part=0, parts=1):
+            by4(engine, h_by4, (g, n), h_t[g], n, part, parts)
 
         def quant_h(g, n):
-            nc.vector.quantize_mx(
-                out=h_codes[:, g, half(n)].bitcast(E4M3),
-                scales=h_scales[:, g, half(n)],
-                in_=h_by4[g, n][:].rearrange("p i j -> p (i j)"),
-            )
+            cols = span(2 * g + n, HALF)
+            nc.vector.quantize_mx(out=h_codes[:, cols].bitcast(E4M3), scales=h_scales[:, cols], in_=h_by4[g, n][:])
 
         def mask_w(f, n):
-            nc.vector.tensor_tensor(
-                out=w_t[f][:, :, half(n)], in0=w_t[f][:, :, half(n)], in1=mask[:, f, :, half(n)], op=MULT
-            )
+            rows = w_t[f][:].rearrange("q (t i) -> q t i", t=PACK)[:, :, span(n, HALF)]
+            keeps = mask[:, span(f, PACK * INS)].rearrange("q (t i) -> q t i", t=PACK)[:, :, span(n, HALF)]
+            nc.vector.tensor_tensor(out=rows, in0=rows, in1=keeps, op=MULT)
 
         def spread_w(f, n, engine="s"):
-            w_by4[f, n] = by4(engine, w_t[f][:, :, half(n)])
+            by4(engine, w_by4, (f, n), w_t[f], n, 0, 1)
 
         def quant_w(f, n):
-            nc.vector.quantize_mx(
-                out=w_codes[:, f, half(n)].bitcast(E4M3),
-                scales=w_scales[:, f, half(n)],
-                in_=w_by4[f, n][:].rearrange("q i t -> q (i t)"),
-            )
+            cols = span(2 * f + n, HALF)
+            nc.vector.quantize_mx(out=w_codes[:, cols].bitcast(E4M3), scales=w_scales[:, cols], in_=w_by4[f, n][:])
 
-        def dx(g, j, engines="ss"):
-            pair, k = divmod(j, 2)
-            if (g, pair) not in dx_t:
-                new = pool.tile([P, 2, INS], F32, tag="result", bufs=4, name="dx_tile")
-                dx_t[g, pair] = new
-            cols = slice(j * P, (j + 1) * P)
-            banks = []
+        def dx(g, j):
+            a, k = divmod(j, 2)
             for n in range(2):
-                bank = psum.tile([P, HALF], F32, tag="dx", name="dx_bank")
+                new = next_bank()
                 for f in range(2):
                     nc.tensor.matmul_mx(
-                        out=bank[:],
-                        lhsT=z_feat_codes[g][:, f, cols].bitcast(E5M2),
-                        lhsT_scale=z_feat_scales[g][:, f, cols],
-                        rhs=w_codes[:, f, half(n)].bitcast(E4M3),
-                        rhs_scale=w_scales[:, f, half(n)],
+                        out=new[:],
+                        lhsT=feat_codes[g, a][:, span(2 * f + k, P)].bitcast(E5M2),
+                        lhsT_scale=feat_scales[g, a][:, span(2 * f + k, P)],
+                        rhs=w_codes[:, span(2 * f + n, HALF)].bitcast(E4M3),
+                        rhs_scale=w_scales[:, span(2 * f + n, HALF)],
                         start=(f == 0),
                         stop=(f == 1),
                     )
-                banks.append(bank)
+                dx_bank[g, j, n] = new
+
+        def dx_out(g, j, engines="ss"):
+            a, k = divmod(j, 2)
+            if k == 0:
+                new = keep.tile([P, PAIR], F32, tag="pre%d%d" % (g, a), name="dx_tile")
+                dx_t[g, a] = new
             for n in range(2):
-                move(engines[n], dx_t[g, pair][:, k, half(n)], banks[n][:])
+                move(engines[n], dx_t[g, a][:, span(2 * k + n, HALF)], dx_bank[g, j, n][:])
 
-        def store_dx(g, pair):
-            nc.sync.dma_start(out=dx_v[g, :, 2 * pair : 2 * pair + 2, :], in_=dx_t[g, pair][:])
+        def store_dx(g, a):
+            nc.sync.dma_start(out=dx_v[g, :, span(a, PAIR)], in_=dx_t[g, a][:])
 
-        def dw(f, t, *groups):
-            cols = slice(f * HALF + t * P, f * HALF + (t + 1) * P)
-            for g in groups:
-                for n in range(2):
-                    if g == 0:
-                        tag = "turn" if (f, t) in IN_TURN_BANKS else "dw" + str(n)
-                        bank = psum.tile([P, HALF], F32, tag=tag, name="dw_bank")
-                        dw_acc[f, t, n] = bank
-                    nc.tensor.matmul_mx(
-                        out=dw_acc[f, t, n][:],
-                        lhsT=z_tok_codes[:, g, cols].bitcast(E5M2),
-                        lhsT_scale=z_tok_scales[:, g, cols],
-                        rhs=h_codes[:, g, half(n)].bitcast(E4M3),
-                        rhs_scale=h_scales[:, g, half(n)],
-                        start=(g == 0),
-                        stop=(g == GROUPS - 1),
-                    )
+        def dw(f, t, n, g):
+            if g == 0:
+                dw_bank[f, t, n] = next_bank()
+            cols = span(8 * g + 4 * f + t, P)
+            nc.tensor.matmul_mx(
+                out=dw_bank[f, t, n][:],
+                lhsT=z_tok_codes[:, cols].bitcast(E5M2),
+                lhsT_scale=z_tok_scales[:, cols],
+                rhs=h_codes[:, span(2 * g + n, HALF)].bitcast(E4M3),
+                rhs_scale=h_scales[:, span(2 * g + n, HALF)],
+                start=(g == 0),
+                stop=(g == LAST),
+            )
 
-        def out_dw(f, t, stores=1):
-            new = pool.tile([P, INS], F32, tag="result", bufs=4, name="dw_tile")
+        def dw_out(f, t):
+            a, k = divmod(t, 2)
+            if k == 0:
+                new = pool.tile([P, PAIR], F32, tag="rows", bufs=4, name="dw_tile")
+                dw_t[f, a] = new
             for n in range(2):
                 nc.vector.tensor_tensor(
-                    out=new[:, half(n)], in0=dw_acc[f, t, n][:], in1=mask[:, f, t, half(n)], op=MULT
+                    out=dw_t[f, a][:, span(2 * k + n, HALF)],
+                    in0=dw_bank[f, t, n][:],
+                    in1=mask[:, span(8 * f + 2 * t + n, HALF)],
+                    op=MULT,
                 )
-                if stores == 2:
-                    nc.sync.dma_start(out=dw_v[f, :, t, half(n)], in_=new[:, half(n)])
-            if stores == 1:
-                nc.sync.dma_start(out=dw_v[f, :, t, :], in_=new[:])
+
+        def store_dw(f, a, cols=slice(0, PAIR)):
+            nc.sync.dma_start(out=dw_v[f, :, span(a, PAIR)][:, cols], in_=dw_t[f, a][:, cols])
+
+        def dx_pair(g, a, engines="ss"):
+            for j in (2 * a, 2 * a + 1):
+                dx(g, j)
+                dx_out(g, j, engines)
+
+        def load_group(g):
+            load_grad(g)
+            load_pre(g, 0)
+            load_pre(g, 1)
 
         with tc.manual_schedule():
-            load_w(0)
-            load_mask(0)
-            load_grad(0, cols=half(0), rows=slice(0, 2))
-            mask_w(0, 0)
-            load_pre(0, cols=half(0), rows=slice(0, 2))
-            mask_w(0, 1)
-            load_grad(0, cols=half(1))
-            spread_w(0, 0, "v")
-            load_pre(0, cols=half(1))
-            gate(0, 0, rows=slice(0, 2))
-            quant_w(0, 0)
-            load_pre(0, cols=half(0), rows=slice(2, 4))
-            load_grad(0, cols=half(0), rows=slice(2, 4))
-            spread_w(0, 1)
-            quant_w(0, 1)
+            for a in range(2):
+                load_w(a)
+                load_grad(0, span(a, PAIR))
+                load_pre(0, a)
+            for g in range(1, GROUPS):
+                load_group(g)
             load_h(0)
-            gate(0, 1)
-            load_w(1)
-            gate(0, 0, rows=slice(2, 4))
-            spread_dz(0, 1)
-            turn(0, 1)
-            spread_dz(0, 0)
-            spread_h(0, 0)
-            quant_tok(0, 0)
-            load_mask(1)
+            load_h(1)
+
+            mask_w(0, 0)
+            spread_w(0, 0)
+            mask_w(0, 1)
+            spread_w(0, 1)
+            gate(0, 0)
             turn(0, 0)
-            quant_h(0, 0)
-            load_grad(1)
-            quant_feat(0, 0)
+            turn_out(0, 0)
+            quant_w(0, 0)
+            quant_w(0, 1)
             mask_w(1, 0)
-            spread_h(0, 1)
             spread_w(1, 0)
             mask_w(1, 1)
-            quant_feat(0, 1)
-            spread_w(1, 1, "v")
-            quant_w(1, 0)
-            quant_w(1, 1)
-            load_pre(1)
-            dx(0, 0)
-            quant_h(0, 1)
+            spread_w(1, 1)
             load_h(2)
-            quant_tok(0, 1)
-            gate(1, 0)
-            dx(0, 2)
-            gate(1, 1)
-            spread_h(2, 1, "v")
-            spread_h(2, 0)
-            spread_dz(1, 0)
-            load_h(1)
-            turn(1, 0)
-            load_grad(2)
-            dx(0, 3)
-            quant_feat(1, 0)
-            dw(0, 1, 0)
-            quant_h(2, 1)
-            turn(1, 1)
-            spread_h(1, 1)
-            dw(0, 0, 0)
-            quant_feat(1, 1)
-            dx(1, 2)
-            spread_h(1, 0)
-            quant_tok(1, 0)
-            quant_h(2, 0)
-            load_pre(2)
-            quant_h(1, 1)
-            gate(2, 0)
-            dx(1, 0)
-            gate(2, 1)
-            turn(2, 0)
-            dx(1, 1)
-            load_pre(3)
-            spread_dz(2, 0)
-            load_grad(3)
-            turn(2, 1)
-            quant_h(1, 0)
             load_h(3)
-            dx(0, 1)
-            dw(0, 1, 1)
-            quant_feat(2, 0)
-            spread_h(3, 1)
-            quant_tok(2, 0)
-            store_dx(0, 1)
-            store_dx(0, 0)
-            dw(0, 0, 1)
-            dw(0, 1, 2)
-            dx(1, 3)
-            gate(3, 1)
-            turn(3, 1)
-            store_dx(1, 1)
-            quant_feat(2, 1)
-            dw(0, 0, 2)
-            gate(3, 0)
-            dx(2, 2)
+
+            for s in range(1, 2 * GROUPS):
+                g, a = divmod(s, 2)
+                before = divmod(s - 1, 2)
+                if s == 1:
+                    quant_feat(*before)
+                gate(g, a)
+                turn(g, a)
+                turn_out(g, a)
+                if s == 1:
+                    quant_w(1, 0)
+                else:
+                    quant_feat(*before)
+                if a == 1:
+                    spread_dz(g, 0)
+                else:
+                    quant_tok(g - 1, 0)
+                if s == 1:
+                    quant_w(1, 1)
+                dx_pair(*before)
+            spread_h(0, 0, "v")
+            quant_feat(LAST, 1)
+            dx_pair(LAST, 1)
+            for g in range(GROUPS):
+                for a in range(2):
+                    store_dx(g, a)
+            quant_tok(LAST, 0)
+            spread_h(0, 1, "v")
+            quant_h(0, 0)
+            spread_h(1, 0, "v")
+            quant_h(0, 1)
+            spread_h(1, 1, "s")
+            quant_h(1, 0)
+            spread_h(2, 0, "v")
+            quant_h(1, 1)
+            spread_h(2, 1, "s")
+            quant_h(2, 0)
             spread_h(3, 0, "v")
-            spread_dz(3, 0)
-            turn(3, 0)
+            quant_h(2, 1)
+            spread_h(3, 1, "s")
             quant_h(3, 0)
-            dx(2, 3)
-            store_dx(1, 0)
-            store_dx(2, 1)
-            dw(1, 2, 0)
-            quant_tok(3, 0)
-            dx(2, 0)
+            spread_dz(0, 1, "v")
             quant_h(3, 1)
-            quant_feat(3, 1)
-            dw(0, 1, 3)
-            dx(2, 1)
-            out_dw(0, 1)
-            quant_feat(3, 0)
-            store_dx(2, 0)
-            dw(0, 0, 3)
-            dw(0, 2, 0)
-            spread_dz(1, 1)
-            spread_dz(2, 1)
-            quant_tok(1, 1)
-            out_dw(0, 0)
-            dx(3, 2)
-            dw(0, 2, 1, 2)
-            dx(3, 3)
-            dw(0, 2, 3)
-            out_dw(0, 2)
-            quant_tok(2, 1)
-            dx(3, 0)
-            dw(0, 3, 0)
-            spread_dz(3, 1)
-            dw(1, 2, 1)
-            dw(1, 0, 0)
-            store_dx(3, 1)
-            dw(1, 0, 1)
-            quant_tok(3, 1)
-            dw(1, 0, 2)
-            dx(3, 1, "vv")
-            dw(0, 3, 1)
-            dw(1, 2, 2, 3)
-            dw(0, 3, 2, 3)
-            store_dx(3, 0)
-            dw(1, 0, 3)
-            out_dw(1, 2)
-            dw(1, 1, 0, 1, 2, 3)
-            out_dw(0, 3)
-            out_dw(1, 0)
-            dw(1, 3, 0, 1)
-            out_dw(1, 1)
-            dw(1, 3, 2, 3)
-            out_dw(1, 3, stores=2)
+            for g in range(GROUPS):
+                for t in range(PACK):
+                    for n in range(2):
+                        dw(0, t, n, g)
+            for t in range(PACK):
+                if t < LAST:
+                    spread_dz(t + 1, 1, "s")
+                dw_out(0, t)
+                quant_tok(t, 1)
+                if t % 2:
+                    store_dw(0, t // 2)
+                if t < LAST:
+                    for g in range(t):
+                        for n in range(2):
+                            dw(1, t, n, g)
+                    for tile in range(t + 1):
+                        for n in range(2):
+                            dw(1, tile, n, t)
+            for t in range(PACK):
+                for g in range(GROUPS) if t == LAST else [LAST]:
+                    for n in range(2):
+                        dw(1, t, n, g)
+                dw_out(1, t)
+                store_dw(1, t // 2, span(t % 2, INS))

@@ -125,16 +125,11 @@ def tile_scm_mlp_pa_v_kernel(tc, h_in, w, masks, mu, sigma, z, pre, grad_out, ou
         def spread_dz(g, f, engine="v"):
             new = pool.tile([P, PACK * HALF], BF16, tag="tok_by4", bufs=3, align_bytes=64, name="tok_tile")
             src = dz_t[g][:].rearrange("p (j w) -> p j w", j=PACK)[:, :, span(f, HALF)]
-            if engine == "v":
-                nc.vector.tensor_copy(
-                    out=new[:].rearrange("p (t q j) -> p q t j", t=PACK, j=PACK),
-                    in_=src.rearrange("p j (q t) -> p q t j", t=PACK),
-                )
-            else:
-                nc.scalar.copy(
-                    out=new[:].rearrange("p (t c r j) -> p c t j r", t=PACK, r=2, j=PACK),
-                    in_=src.rearrange("p j (c r t) -> p c t j r", r=2, t=PACK),
-                )
+            move(
+                engine,
+                new[:].rearrange("p (t c r j) -> p c j r t", t=PACK, r=2, j=PACK),
+                src.rearrange("p j (c r t) -> p c j r t", r=2, t=PACK),
+            )
             tok_by4[g, f] = new
 
         def quant_tok(g, f):

@@ -22,13 +22,14 @@ HALF = P * PACK
 GROUPS = TOKENS // HALF
 LAST = GROUPS - 1
 PAIR = 2 * FEATS
+ROWS = PACK * INS
 
 
 def tile_scm_mlp_pa_v_kernel(tc, h_in, w, masks, mu, sigma, z, pre, grad_out, out_0, out_1):
     nc = tc.nc
     pre_v = pre.rearrange("(g p j) w -> g p (j w)", p=P, j=PACK)
     grad_v = grad_out.rearrange("(g p j) w -> g p (j w)", p=P, j=PACK)
-    h_v = h_in.rearrange("(g p j) i -> g p (j i)", p=P, j=PACK)
+    h_v = h_in.rearrange("(g p j) i -> p g (j i)", p=P, j=PACK)
     w_v = w[0, :, :].rearrange("(f q t) i -> f q (t i)", q=P, t=PACK)
     mask_v = masks[0, :, :].rearrange("(f q t) i -> f q (t i)", q=P, t=PACK)
     dx_v = out_0.rearrange("(g p j) i -> g p (j i)", p=P, j=PACK)
@@ -53,6 +54,8 @@ def tile_scm_mlp_pa_v_kernel(tc, h_in, w, masks, mu, sigma, z, pre, grad_out, ou
         w_scales = keep.tile([P, 2 * INS], U8, align_bytes=64, name="w_scales")
         mask = keep.tile([P, 2 * PACK * INS], BF16, align_bytes=64, name="mask")
 
+        w_all = pool.tile([P, 2 * ROWS], BF16, tag="rows", name="w_all")
+
         pre_t, dz_t, h_t, w_t = {}, {}, {}, {}
         tok_by4, feat_by4, h_by4, w_by4 = {}, {}, {}, {}
         feat_codes, feat_scales = {}, {}
@@ -68,9 +71,10 @@ def tile_scm_mlp_pa_v_kernel(tc, h_in, w, masks, mu, sigma, z, pre, grad_out, ou
             return psum.tile([P, HALF], F32, tag="bank", bufs=8, name="bank_tile")
 
         def load_pre(g, a):
-            new = keep.tile([P, PAIR], F32, tag="pre%d%d" % (g, a), name="pre_tile")
-            nc.sync.dma_start(out=new[:], in_=pre_v[g, :, span(a, PAIR)])
-            pre_t[g, a] = new
+            if a == 0:
+                new = keep.tile([P, 2 * PAIR], F32, tag="pre%d" % g, name="pre_tile")
+                pre_t[g] = new
+            nc.sync.dma_start(out=pre_t[g][:, span(a, PAIR)], in_=pre_v[g, :, span(a, PAIR)])
 
         def load_grad(g, cols=slice(0, 2 * PAIR)):
             if g not in dz_t:
@@ -79,19 +83,21 @@ def tile_scm_mlp_pa_v_kernel(tc, h_in, w, masks, mu, sigma, z, pre, grad_out, ou
             nc.sync.dma_start(out=dz_t[g][:, cols], in_=grad_v[g, :, cols])
 
         def load_h(g):
-            new = pool.tile([P, PACK * INS], BF16, tag="rows", bufs=4, name="h_tile")
-            nc.sync.dma_start(out=new[:], in_=h_v[g, :, :])
-            h_t[g] = new
+            new = pool.tile([P, 2 * ROWS], BF16, tag="rows", name="h_tile")
+            nc.sync.dma_start(out=new[:].rearrange("p (g c) -> p g c", g=2), in_=h_v[:, g : g + 2, :])
+            for k in range(2):
+                h_t[g + k] = new[:, span(k, ROWS)]
 
         def load_w(f):
-            new = pool.tile([P, PACK * INS], BF16, tag="rows", bufs=4, name="w_tile")
-            nc.sync.dma_start(out=new[:], in_=w_v[f, :, :])
-            nc.sync.dma_start(out=mask[:, span(f, PACK * INS)], in_=mask_v[f, :, :])
-            w_t[f] = new
+            nc.sync.dma_start(out=w_all[:, span(f, ROWS)], in_=w_v[f, :, :])
+            nc.sync.dma_start(out=mask[:, span(f, ROWS)], in_=mask_v[f, :, :])
+            w_t[f] = w_all[:, span(f, ROWS)]
 
         def gate(g, a):
             rows = dz_t[g][:, span(a, PAIR)]
-            nc.vector.scalar_tensor_tensor(out=rows, in0=pre_t[g, a][:], scalar=0.0, in1=rows, op0=IS_GT, op1=MULT)
+            nc.vector.scalar_tensor_tensor(
+                out=rows, in0=pre_t[g][:, span(a, PAIR)], scalar=0.0, in1=rows, op0=IS_GT, op1=MULT
+            )
 
         def turn(g, a):
             words = dz_t[g][:].bitcast(F32)
@@ -143,7 +149,7 @@ def tile_scm_mlp_pa_v_kernel(tc, h_in, w, masks, mu, sigma, z, pre, grad_out, ou
                 new = pool.tile([P, PACK * HALF], BF16, tag="by4", bufs=3, align_bytes=64, name="by4_tile")
                 tiles[key] = new
             width = HALF // parts
-            src = rows[:].rearrange("p (t i) -> p t i", t=PACK)[:, :, span(n * parts + part, width)]
+            src = rows.rearrange("p (t i) -> p t i", t=PACK)[:, :, span(n * parts + part, width)]
             move(
                 engine,
                 tiles[key][:, span(part, PACK * width)].rearrange("p (c i t) -> p c t i", i=4, t=PACK),
@@ -158,8 +164,8 @@ def tile_scm_mlp_pa_v_kernel(tc, h_in, w, masks, mu, sigma, z, pre, grad_out, ou
             nc.vector.quantize_mx(out=h_codes[:, cols].bitcast(E4M3), scales=h_scales[:, cols], in_=h_by4[g, n][:])
 
         def mask_w(f, n):
-            rows = w_t[f][:].rearrange("q (t i) -> q t i", t=PACK)[:, :, span(n, HALF)]
-            keeps = mask[:, span(f, PACK * INS)].rearrange("q (t i) -> q t i", t=PACK)[:, :, span(n, HALF)]
+            rows = w_t[f].rearrange("q (t i) -> q t i", t=PACK)[:, :, span(n, HALF)]
+            keeps = mask[:, span(f, ROWS)].rearrange("q (t i) -> q t i", t=PACK)[:, :, span(n, HALF)]
             nc.vector.tensor_tensor(out=rows, in0=rows, in1=keeps, op=MULT)
 
         def spread_w(f, n, engine="s"):
@@ -186,15 +192,14 @@ def tile_scm_mlp_pa_v_kernel(tc, h_in, w, masks, mu, sigma, z, pre, grad_out, ou
                 dx_bank[g, j, n] = new
 
         def dx_out(g, j, engines="ss"):
-            a, k = divmod(j, 2)
-            if k == 0:
-                new = keep.tile([P, PAIR], F32, tag="pre%d%d" % (g, a), name="dx_tile")
-                dx_t[g, a] = new
+            if j == 0:
+                new = keep.tile([P, 2 * PAIR], F32, tag="pre%d" % g, name="dx_tile")
+                dx_t[g] = new
             for n in range(2):
-                move(engines[n], dx_t[g, a][:, span(2 * k + n, HALF)], dx_bank[g, j, n][:])
+                move(engines[n], dx_t[g][:, span(2 * j + n, HALF)], dx_bank[g, j, n][:])
 
-        def store_dx(g, a):
-            nc.sync.dma_start(out=dx_v[g, :, span(a, PAIR)], in_=dx_t[g, a][:])
+        def store_dx(g):
+            nc.sync.dma_start(out=dx_v[g, :, :], in_=dx_t[g][:])
 
         def dw(f, t, n, g):
             if g == 0:
@@ -210,21 +215,20 @@ def tile_scm_mlp_pa_v_kernel(tc, h_in, w, masks, mu, sigma, z, pre, grad_out, ou
                 stop=(g == LAST),
             )
 
-        def dw_out(f, t):
-            a, k = divmod(t, 2)
-            if k == 0:
-                new = pool.tile([P, PAIR], F32, tag="rows", bufs=4, name="dw_tile")
-                dw_t[f, a] = new
-            for n in range(2):
+        def dw_out(f, t, halves=range(2)):
+            if f not in dw_t:
+                new = pool.tile([P, ROWS], F32, tag="rows", name="dw_tile")
+                dw_t[f] = new
+            for n in halves:
                 nc.vector.tensor_tensor(
-                    out=dw_t[f, a][:, span(2 * k + n, HALF)],
+                    out=dw_t[f][:, span(2 * t + n, HALF)],
                     in0=dw_bank[f, t, n][:],
                     in1=mask[:, span(8 * f + 2 * t + n, HALF)],
                     op=MULT,
                 )
 
-        def store_dw(f, a, cols=slice(0, PAIR)):
-            nc.sync.dma_start(out=dw_v[f, :, span(a, PAIR)][:, cols], in_=dw_t[f, a][:, cols])
+        def store_dw(f, cols):
+            nc.sync.dma_start(out=dw_v[f, :, cols], in_=dw_t[f][:, cols])
 
         def dx_pair(g, a, engines="ss"):
             for j in (2 * a, 2 * a + 1):
@@ -244,7 +248,6 @@ def tile_scm_mlp_pa_v_kernel(tc, h_in, w, masks, mu, sigma, z, pre, grad_out, ou
             for g in range(1, GROUPS):
                 load_group(g)
             load_h(0)
-            load_h(1)
 
             mask_w(0, 0)
             spread_w(0, 0)
@@ -260,7 +263,6 @@ def tile_scm_mlp_pa_v_kernel(tc, h_in, w, masks, mu, sigma, z, pre, grad_out, ou
             mask_w(1, 1)
             spread_w(1, 1)
             load_h(2)
-            load_h(3)
 
             for s in range(1, 2 * GROUPS):
                 g, a = divmod(s, 2)
@@ -285,8 +287,7 @@ def tile_scm_mlp_pa_v_kernel(tc, h_in, w, masks, mu, sigma, z, pre, grad_out, ou
             quant_feat(LAST, 1)
             dx_pair(LAST, 1)
             for g in range(GROUPS):
-                for a in range(2):
-                    store_dx(g, a)
+                store_dx(g)
             quant_tok(LAST, 0)
             spread_h(0, 1, "v")
             quant_h(0, 0)
@@ -314,7 +315,7 @@ def tile_scm_mlp_pa_v_kernel(tc, h_in, w, masks, mu, sigma, z, pre, grad_out, ou
                 dw_out(0, t)
                 quant_tok(t, 1)
                 if t % 2:
-                    store_dw(0, t // 2)
+                    store_dw(0, span(t // 2, PAIR))
                 if t < LAST:
                     for g in range(t):
                         for n in range(2):
@@ -327,4 +328,4 @@ def tile_scm_mlp_pa_v_kernel(tc, h_in, w, masks, mu, sigma, z, pre, grad_out, ou
                     for n in range(2):
                         dw(1, t, n, g)
                 dw_out(1, t)
-                store_dw(1, t // 2, span(t % 2, INS))
+                store_dw(1, span(t, INS))

@@ -21,6 +21,7 @@ PACK = 4
 HALF = P * PACK
 GROUPS = TOKENS // HALF
 LAST = GROUPS - 1
+BANKS = 8
 PAIR = 2 * FEATS
 ROWS = PACK * INS
 
@@ -57,7 +58,7 @@ def tile_scm_mlp_pa_v_kernel(tc, h_in, w, masks, mu, sigma, z, pre, grad_out, ou
         w_all = pool.tile([P, 2 * ROWS], BF16, tag="rows", name="w_all")
 
         pre_t, dz_t, h_t, w_t = {}, {}, {}, {}
-        tok_by4, feat_by4, h_by4, w_by4 = {}, {}, {}, {}
+        masked, tok_by4, feat_by4, h_by4, w_by4 = {}, {}, {}, {}, {}
         feat_codes, feat_scales = {}, {}
         turn_bank, dx_bank, dx_t, dw_bank, dw_t = {}, {}, {}, {}, {}
 
@@ -67,8 +68,14 @@ def tile_scm_mlp_pa_v_kernel(tc, h_in, w, masks, mu, sigma, z, pre, grad_out, ou
             else:
                 nc.vector.tensor_copy(out=out, in_=in_)
 
+        def bank(b):
+            return psum.tile([P, HALF], F32, tag="bank%d" % b, name="bank_tile")
+
+        taken = []
+
         def next_bank():
-            return psum.tile([P, HALF], F32, tag="bank", bufs=8, name="bank_tile")
+            taken.append(len(taken) % BANKS)
+            return bank(taken[-1])
 
         def load_pre(g, a):
             if a == 0:
@@ -129,7 +136,7 @@ def tile_scm_mlp_pa_v_kernel(tc, h_in, w, masks, mu, sigma, z, pre, grad_out, ou
             feat_codes[g, a], feat_scales[g, a] = codes, scales
 
         def spread_dz(g, f, engine="v"):
-            new = pool.tile([P, PACK * HALF], BF16, tag="tok_by4", bufs=3, align_bytes=64, name="tok_tile")
+            new = pool.tile([P, PACK * HALF], BF16, tag="by4", bufs=6, align_bytes=64, name="tok_tile")
             src = dz_t[g][:].rearrange("p (j w) -> p j w", j=PACK)[:, :, span(f, HALF)]
             move(
                 engine,
@@ -144,20 +151,13 @@ def tile_scm_mlp_pa_v_kernel(tc, h_in, w, masks, mu, sigma, z, pre, grad_out, ou
                 out=z_tok_codes[:, cols].bitcast(E5M2), scales=z_tok_scales[:, cols], in_=tok_by4[g, f][:]
             )
 
-        def by4(engine, tiles, key, rows, n, part, parts):
-            if part == 0:
-                new = pool.tile([P, PACK * HALF], BF16, tag="by4", bufs=3, align_bytes=64, name="by4_tile")
-                tiles[key] = new
-            width = HALF // parts
-            src = rows.rearrange("p (t i) -> p t i", t=PACK)[:, :, span(n * parts + part, width)]
-            move(
-                engine,
-                tiles[key][:, span(part, PACK * width)].rearrange("p (c i t) -> p c t i", i=4, t=PACK),
-                src.rearrange("p t (c i) -> p c t i", i=4),
-            )
+        def by4(engine, src):
+            new = pool.tile([P, PACK * HALF], BF16, tag="by4", bufs=6, align_bytes=64, name="by4_tile")
+            move(engine, new[:].rearrange("p (c i t) -> p c t i", i=4, t=PACK), src.rearrange("p t (c i) -> p c t i", i=4))
+            return new
 
-        def spread_h(g, n, engine="s", part=0, parts=1):
-            by4(engine, h_by4, (g, n), h_t[g], n, part, parts)
+        def spread_h(g, n, engine="s"):
+            h_by4[g, n] = by4(engine, h_t[g].rearrange("p (j i) -> p j i", j=PACK)[:, :, span(n, HALF)])
 
         def quant_h(g, n):
             cols = span(2 * g + n, HALF)
@@ -166,44 +166,43 @@ def tile_scm_mlp_pa_v_kernel(tc, h_in, w, masks, mu, sigma, z, pre, grad_out, ou
         def mask_w(f, n):
             rows = w_t[f].rearrange("q (t i) -> q t i", t=PACK)[:, :, span(n, HALF)]
             keeps = mask[:, span(f, ROWS)].rearrange("q (t i) -> q t i", t=PACK)[:, :, span(n, HALF)]
-            nc.vector.tensor_tensor(out=rows, in0=rows, in1=keeps, op=MULT)
+            new = pool.tile([P, PACK * HALF], BF16, tag="by4", bufs=6, align_bytes=64, name="masked_tile")
+            nc.vector.tensor_tensor(out=new[:].rearrange("q (t i) -> q t i", t=PACK), in0=rows, in1=keeps, op=MULT)
+            masked[f, n] = new
 
         def spread_w(f, n, engine="s"):
-            by4(engine, w_by4, (f, n), w_t[f], n, 0, 1)
+            w_by4[f, n] = by4(engine, masked[f, n][:].rearrange("q (t i) -> q t i", t=PACK))
 
         def quant_w(f, n):
             cols = span(2 * f + n, HALF)
             nc.vector.quantize_mx(out=w_codes[:, cols].bitcast(E4M3), scales=w_scales[:, cols], in_=w_by4[f, n][:])
 
-        def dx(g, j):
+        def dx(g, j, n, f):
             a, k = divmod(j, 2)
-            for n in range(2):
-                new = next_bank()
-                for f in range(2):
-                    nc.tensor.matmul_mx(
-                        out=new[:],
-                        lhsT=feat_codes[g, a][:, span(2 * f + k, P)].bitcast(E5M2),
-                        lhsT_scale=feat_scales[g, a][:, span(2 * f + k, P)],
-                        rhs=w_codes[:, span(2 * f + n, HALF)].bitcast(E4M3),
-                        rhs_scale=w_scales[:, span(2 * f + n, HALF)],
-                        start=(f == 0),
-                        stop=(f == 1),
-                    )
-                dx_bank[g, j, n] = new
+            if f == 0:
+                dx_bank[g, j, n] = next_bank()
+            nc.tensor.matmul_mx(
+                out=dx_bank[g, j, n][:],
+                lhsT=feat_codes[g, a][:, span(2 * f + k, P)].bitcast(E5M2),
+                lhsT_scale=feat_scales[g, a][:, span(2 * f + k, P)],
+                rhs=w_codes[:, span(2 * f + n, HALF)].bitcast(E4M3),
+                rhs_scale=w_scales[:, span(2 * f + n, HALF)],
+                start=(f == 0),
+                stop=(f == 1),
+            )
 
-        def dx_out(g, j, engines="ss"):
-            if j == 0:
+        def dx_out(g, j, n):
+            if g not in dx_t:
                 new = keep.tile([P, 2 * PAIR], F32, tag="pre%d" % g, name="dx_tile")
                 dx_t[g] = new
-            for n in range(2):
-                move(engines[n], dx_t[g][:, span(2 * j + n, HALF)], dx_bank[g, j, n][:])
+            nc.scalar.copy(out=dx_t[g][:, span(2 * j + n, HALF)], in_=dx_bank[g, j, n][:])
 
         def store_dx(g):
             nc.sync.dma_start(out=dx_v[g, :, :], in_=dx_t[g][:])
 
         def dw(f, t, n, g):
             if g == 0:
-                dw_bank[f, t, n] = next_bank()
+                dw_bank[f, t, n] = bank(PACK * n + t)
             cols = span(8 * g + 4 * f + t, P)
             nc.tensor.matmul_mx(
                 out=dw_bank[f, t, n][:],
@@ -230,59 +229,88 @@ def tile_scm_mlp_pa_v_kernel(tc, h_in, w, masks, mu, sigma, z, pre, grad_out, ou
         def store_dw(f, cols):
             nc.sync.dma_start(out=dw_v[f, :, cols], in_=dw_t[f][:, cols])
 
-        def dx_pair(g, a, engines="ss"):
+        def dx_pair(g, a):
             for j in (2 * a, 2 * a + 1):
-                dx(g, j)
-                dx_out(g, j, engines)
+                for n in range(2):
+                    for f in range(2):
+                        dx(g, j, n, f)
+                    dx_out(g, j, n)
+
+        def dx_first(n, f):
+            for j in range(PACK):
+                dx(0, j, n, f)
+                if f == 1:
+                    dx_out(0, j, n)
 
         def load_group(g):
             load_grad(g)
             load_pre(g, 0)
             load_pre(g, 1)
 
+        def dw_first(g, n):
+            quant_h(g, n)
+            for t in range(PACK):
+                dw(0, t, n, g)
+
+        def dw_tile(f, t, groups):
+            for g in groups:
+                for n in range(2):
+                    dw(f, t, n, g)
+
         with tc.manual_schedule():
             for a in range(2):
-                load_w(a)
                 load_grad(0, span(a, PAIR))
                 load_pre(0, a)
+            for f in range(2):
+                load_w(f)
             for g in range(1, GROUPS):
                 load_group(g)
             load_h(0)
-
+            gate(0, 0)
+            turn(0, 0)
+            turn_out(0, 0)
+            gate(0, 1)
+            turn(0, 1)
+            quant_feat(0, 0)
+            spread_dz(0, 1, "s")
+            spread_dz(0, 0)
+            turn_out(0, 1)
             mask_w(0, 0)
             spread_w(0, 0)
             mask_w(0, 1)
             spread_w(0, 1)
-            gate(0, 0)
-            turn(0, 0)
-            turn_out(0, 0)
-            quant_w(0, 0)
-            quant_w(0, 1)
+            quant_tok(0, 0)
+            quant_feat(0, 1)
+            quant_tok(0, 1)
             mask_w(1, 0)
             spread_w(1, 0)
+            quant_w(0, 0)
+            dx_first(0, 0)
             mask_w(1, 1)
             spread_w(1, 1)
             load_h(2)
-
-            for s in range(1, 2 * GROUPS):
+            quant_w(0, 1)
+            dx_first(1, 0)
+            quant_w(1, 0)
+            dx_first(0, 1)
+            for s in range(2, 2 * GROUPS):
                 g, a = divmod(s, 2)
                 before = divmod(s - 1, 2)
-                if s == 1:
-                    quant_feat(*before)
                 gate(g, a)
+                if s == 2:
+                    quant_w(1, 1)
                 turn(g, a)
                 turn_out(g, a)
-                if s == 1:
-                    quant_w(1, 0)
+                if s == 2:
+                    dx_first(1, 1)
                 else:
                     quant_feat(*before)
                 if a == 1:
                     spread_dz(g, 0)
-                else:
+                elif g > 1:
                     quant_tok(g - 1, 0)
-                if s == 1:
-                    quant_w(1, 1)
-                dx_pair(*before)
+                if s > 2:
+                    dx_pair(*before)
             spread_h(0, 0, "v")
             quant_feat(LAST, 1)
             dx_pair(LAST, 1)
@@ -293,39 +321,50 @@ def tile_scm_mlp_pa_v_kernel(tc, h_in, w, masks, mu, sigma, z, pre, grad_out, ou
             quant_h(0, 0)
             spread_h(1, 0, "v")
             quant_h(0, 1)
-            spread_h(1, 1, "s")
+            spread_h(1, 1, "v")
             quant_h(1, 0)
+            spread_h(2, 1, "s")
             spread_h(2, 0, "v")
             quant_h(1, 1)
-            spread_h(2, 1, "s")
+            spread_h(3, 1, "s")
             quant_h(2, 0)
             spread_h(3, 0, "v")
             quant_h(2, 1)
-            spread_h(3, 1, "s")
+            spread_dz(1, 1, "s")
             quant_h(3, 0)
-            spread_dz(0, 1, "v")
             quant_h(3, 1)
-            for g in range(GROUPS):
-                for t in range(PACK):
-                    for n in range(2):
+            for t in range(PACK):
+                dw_tile(0, t, [0])
+            for g in range(1, LAST):
+                for n in range(2):
+                    for t in range(PACK):
                         dw(0, t, n, g)
             for t in range(PACK):
-                if t < LAST:
-                    spread_dz(t + 1, 1, "s")
-                dw_out(0, t)
-                quant_tok(t, 1)
-                if t % 2:
-                    store_dw(0, span(t // 2, PAIR))
-                if t < LAST:
-                    for g in range(t):
-                        for n in range(2):
-                            dw(1, t, n, g)
-                    for tile in range(t + 1):
-                        for n in range(2):
-                            dw(1, tile, n, t)
-            for t in range(PACK):
-                for g in range(GROUPS) if t == LAST else [LAST]:
-                    for n in range(2):
-                        dw(1, t, n, g)
+                dw_tile(0, t, [LAST])
+            spread_dz(2, 1, "s")
+            quant_tok(1, 1)
+            dw_out(0, 0)
+            store_dw(0, span(0, INS))
+            dw_tile(1, 0, [0, 1])
+            spread_dz(3, 1, "s")
+            dw_out(0, 1)
+            store_dw(0, span(1, INS))
+            dw_tile(1, 1, [0, 1])
+            quant_tok(2, 1)
+            dw_out(0, 2)
+            store_dw(0, span(2, INS))
+            dw_tile(1, 0, [2])
+            dw_tile(1, 1, [2])
+            dw_tile(1, 2, [0, 1])
+            quant_tok(3, 1)
+            dw_out(0, 3)
+            store_dw(0, span(3, INS))
+            for t in range(LAST):
+                dw_tile(1, t, [LAST] if t < 2 else [2, LAST])
                 dw_out(1, t)
                 store_dw(1, span(t, INS))
+            for n in range(2):
+                for g in range(GROUPS):
+                    dw(1, LAST, n, g)
+                dw_out(1, LAST, [n])
+            store_dw(1, span(LAST, INS))

@@ -28,12 +28,12 @@ ROWS = PACK * INS
 
 def tile_scm_mlp_pa_v_kernel(tc, h_in, w, masks, mu, sigma, z, pre, grad_out, out_0, out_1):
     nc = tc.nc
-    pre_v = pre.rearrange("(g p j) w -> g p (j w)", p=P, j=PACK)
-    grad_v = grad_out.rearrange("(g p j) w -> g p (j w)", p=P, j=PACK)
+    pre_v = pre.rearrange("(g p j) w -> p g (j w)", p=P, j=PACK)
+    grad_v = grad_out.rearrange("(g p j) w -> p g (j w)", p=P, j=PACK)
     h_v = h_in.rearrange("(g p j) i -> p g (j i)", p=P, j=PACK)
     w_v = w[0, :, :].rearrange("(f q t) i -> f q (t i)", q=P, t=PACK)
     mask_v = masks[0, :, :].rearrange("(f q t) i -> f q (t i)", q=P, t=PACK)
-    dx_v = out_0.rearrange("(g p j) i -> g p (j i)", p=P, j=PACK)
+    dx_v = out_0.rearrange("(g p j) i -> p g (j i)", p=P, j=PACK)
     dw_v = out_1[0, :, :].rearrange("(f q t) i -> f q (t i)", q=P, t=PACK)
 
     def span(k, width):
@@ -47,20 +47,32 @@ def tile_scm_mlp_pa_v_kernel(tc, h_in, w, masks, mu, sigma, z, pre, grad_out, ou
         ident = keep.tile([P, P], F32, name="ident")
         make_identity(nc, ident[:])
 
-        z_tok_codes = keep.tile([P, GROUPS * FEATS], U32, align_bytes=64, name="z_tok_codes")
-        z_tok_scales = keep.tile([P, GROUPS * FEATS], U8, align_bytes=64, name="z_tok_scales")
-        h_codes = keep.tile([P, GROUPS * INS], U32, align_bytes=64, name="h_codes")
-        h_scales = keep.tile([P, GROUPS * INS], U8, align_bytes=64, name="h_scales")
-        w_codes = keep.tile([P, 2 * INS], U32, align_bytes=64, name="w_codes")
-        w_scales = keep.tile([P, 2 * INS], U8, align_bytes=64, name="w_scales")
+        def placed(where, tag, words, dtype, skip, bufs=1):
+            pad = skip if dtype is U8 else skip // 4
+            new = where.tile([P, words + pad], dtype, tag=tag, bufs=bufs, align_bytes=256, name="placed_tile")
+            return new[:, pad : pad + words]
+
+        z_tok_codes = placed(keep, "z_tok_codes", GROUPS * FEATS, U32, 64)
+        z_tok_scales = placed(keep, "z_tok_scales", GROUPS * FEATS, U8, 192)
+        h_codes = placed(keep, "h_codes", GROUPS * INS, U32, 0)
+        h_scales = placed(keep, "h_scales", GROUPS * INS, U8, 128)
+        w_codes = placed(keep, "w_codes", 2 * INS, U32, 0)
+        w_scales = placed(keep, "w_scales", 2 * INS, U8, 128)
         mask = keep.tile([P, 2 * PACK * INS], BF16, align_bytes=64, name="mask")
 
-        w_all = pool.tile([P, 2 * ROWS], BF16, tag="rows", name="w_all")
+        pre_all = keep.tile([P, GROUPS * ROWS], F32, name="pre_all")
+        dz_all = keep.tile([P, GROUPS * ROWS], BF16, align_bytes=64, name="dz_all")
+        pre_t = [pre_all[:, span(g, ROWS)] for g in range(GROUPS)]
+        dz_t = [dz_all[:, span(g, ROWS)] for g in range(GROUPS)]
+        h_all = keep.tile([P, GROUPS * ROWS], BF16, name="h_all")
+        w_all = h_all[:, 2 * ROWS : 4 * ROWS]
+        h_t = [h_all[:, span(g, ROWS)] for g in range(GROUPS)]
+        dw_t = [h_all[:].bitcast(F32)[:, span(f, ROWS)] for f in range(2)]
 
-        pre_t, dz_t, h_t, w_t = {}, {}, {}, {}
+        w_t = {}
         masked, tok_by4, feat_by4, h_by4, w_by4 = {}, {}, {}, {}, {}
         feat_codes, feat_scales = {}, {}
-        turn_bank, dx_bank, dx_t, dw_bank, dw_t = {}, {}, {}, {}, {}
+        turn_bank, dx_bank, dw_bank = {}, {}, {}
 
         def move(engine, out, in_):
             if engine == "s":
@@ -77,37 +89,29 @@ def tile_scm_mlp_pa_v_kernel(tc, h_in, w, masks, mu, sigma, z, pre, grad_out, ou
             taken.append(len(taken) % BANKS)
             return bank(taken[-1])
 
-        def load_pre(g, a):
-            if a == 0:
-                new = keep.tile([P, 2 * PAIR], F32, tag="pre%d" % g, name="pre_tile")
-                pre_t[g] = new
-            nc.sync.dma_start(out=pre_t[g][:, span(a, PAIR)], in_=pre_v[g, :, span(a, PAIR)])
+        def load_pre(g, a, width=PAIR):
+            nc.sync.dma_start(out=pre_t[g][:, span(a, width)], in_=pre_v[:, g, span(a, width)])
 
-        def load_grad(g, cols=slice(0, 2 * PAIR)):
-            if g not in dz_t:
-                new = keep.tile([P, 2 * PAIR], BF16, tag="dz%d" % g, align_bytes=64, name="dz_tile")
-                dz_t[g] = new
-            nc.sync.dma_start(out=dz_t[g][:, cols], in_=grad_v[g, :, cols])
+        def load_grad(g, cols=slice(0, ROWS)):
+            nc.sync.dma_start(out=dz_t[g][:, cols], in_=grad_v[:, g, cols])
 
-        def load_h(g):
-            new = pool.tile([P, 2 * ROWS], BF16, tag="rows", name="h_tile")
-            nc.sync.dma_start(out=new[:].rearrange("p (g c) -> p g c", g=2), in_=h_v[:, g : g + 2, :])
-            for k in range(2):
-                h_t[g + k] = new[:, span(k, ROWS)]
+        def load_h(g, count):
+            rows = h_all[:, g * ROWS : (g + count) * ROWS].rearrange("p (g c) -> p g c", g=count)
+            nc.sync.dma_start(out=rows, in_=h_v[:, g : g + count, :])
 
         def load_w(f):
             nc.sync.dma_start(out=w_all[:, span(f, ROWS)], in_=w_v[f, :, :])
             nc.sync.dma_start(out=mask[:, span(f, ROWS)], in_=mask_v[f, :, :])
             w_t[f] = w_all[:, span(f, ROWS)]
 
-        def gate(g, a):
-            rows = dz_t[g][:, span(a, PAIR)]
+        def gate(g, a, width=PAIR):
+            rows = dz_t[g][:, span(a, width)]
             nc.vector.scalar_tensor_tensor(
-                out=rows, in0=pre_t[g][:, span(a, PAIR)], scalar=0.0, in1=rows, op0=IS_GT, op1=MULT
+                out=rows, in0=pre_t[g][:, span(a, width)], scalar=0.0, in1=rows, op0=IS_GT, op1=MULT
             )
 
         def turn(g, a):
-            words = dz_t[g][:].bitcast(F32)
+            words = dz_t[g].bitcast(F32)
             for f in range(2):
                 new = next_bank()
                 for k in range(2):
@@ -130,14 +134,14 @@ def tile_scm_mlp_pa_v_kernel(tc, h_in, w, masks, mu, sigma, z, pre, grad_out, ou
             feat_by4[g, a] = new
 
         def quant_feat(g, a):
-            codes = pool.tile([P, HALF], U32, tag="feat_codes", bufs=3, align_bytes=64, name="feat_codes_tile")
-            scales = pool.tile([P, HALF], U8, tag="feat_scales", bufs=3, align_bytes=64, name="feat_scales_tile")
-            nc.vector.quantize_mx(out=codes[:].bitcast(E5M2), scales=scales[:], in_=feat_by4[g, a][:])
+            codes = placed(pool, "feat_codes", HALF, U32, 64, bufs=3)
+            scales = placed(pool, "feat_scales", HALF, U8, 192, bufs=3)
+            nc.vector.quantize_mx(out=codes.bitcast(E5M2), scales=scales, in_=feat_by4[g, a][:])
             feat_codes[g, a], feat_scales[g, a] = codes, scales
 
         def spread_dz(g, f, engine="v"):
             new = pool.tile([P, PACK * HALF], BF16, tag="by4", bufs=6, align_bytes=64, name="tok_tile")
-            src = dz_t[g][:].rearrange("p (j w) -> p j w", j=PACK)[:, :, span(f, HALF)]
+            src = dz_t[g].rearrange("p (j w) -> p j w", j=PACK)[:, :, span(f, HALF)]
             move(
                 engine,
                 new[:].rearrange("p (t c r j) -> p c j r t", t=PACK, r=2, j=PACK),
@@ -192,13 +196,11 @@ def tile_scm_mlp_pa_v_kernel(tc, h_in, w, masks, mu, sigma, z, pre, grad_out, ou
             )
 
         def dx_out(g, j, n):
-            if g not in dx_t:
-                new = keep.tile([P, 2 * PAIR], F32, tag="pre%d" % g, name="dx_tile")
-                dx_t[g] = new
-            nc.scalar.copy(out=dx_t[g][:, span(2 * j + n, HALF)], in_=dx_bank[g, j, n][:])
+            nc.scalar.copy(out=pre_t[g][:, span(2 * j + n, HALF)], in_=dx_bank[g, j, n][:])
 
-        def store_dx(g):
-            nc.sync.dma_start(out=dx_v[g, :, :], in_=dx_t[g][:])
+        def store_dx(g, count):
+            rows = pre_all[:, g * ROWS : (g + count) * ROWS].rearrange("p (g c) -> p g c", g=count)
+            nc.sync.dma_start(out=dx_v[:, g : g + count, :], in_=rows)
 
         def dw(f, t, n, g):
             if g == 0:
@@ -215,9 +217,6 @@ def tile_scm_mlp_pa_v_kernel(tc, h_in, w, masks, mu, sigma, z, pre, grad_out, ou
             )
 
         def dw_out(f, t, halves=range(2)):
-            if f not in dw_t:
-                new = pool.tile([P, ROWS], F32, tag="rows", name="dw_tile")
-                dw_t[f] = new
             for n in halves:
                 nc.vector.tensor_tensor(
                     out=dw_t[f][:, span(2 * t + n, HALF)],
@@ -252,6 +251,11 @@ def tile_scm_mlp_pa_v_kernel(tc, h_in, w, masks, mu, sigma, z, pre, grad_out, ou
             for t in range(PACK):
                 dw(0, t, n, g)
 
+        def dw_quarter(f, n, groups):
+            for g in groups:
+                for t in range(PACK):
+                    dw(f, t, n, g)
+
         def dw_tile(f, t, groups):
             for g in groups:
                 for n in range(2):
@@ -265,7 +269,7 @@ def tile_scm_mlp_pa_v_kernel(tc, h_in, w, masks, mu, sigma, z, pre, grad_out, ou
                 load_w(f)
             for g in range(1, GROUPS):
                 load_group(g)
-            load_h(0)
+            load_h(0, 2)
             gate(0, 0)
             turn(0, 0)
             turn_out(0, 0)
@@ -288,7 +292,7 @@ def tile_scm_mlp_pa_v_kernel(tc, h_in, w, masks, mu, sigma, z, pre, grad_out, ou
             dx_first(0, 0)
             mask_w(1, 1)
             spread_w(1, 1)
-            load_h(2)
+            load_h(2, 2)
             quant_w(0, 1)
             dx_first(1, 0)
             quant_w(1, 0)
@@ -314,8 +318,8 @@ def tile_scm_mlp_pa_v_kernel(tc, h_in, w, masks, mu, sigma, z, pre, grad_out, ou
             spread_h(0, 0, "v")
             quant_feat(LAST, 1)
             dx_pair(LAST, 1)
-            for g in range(GROUPS):
-                store_dx(g)
+            store_dx(0, 2)
+            store_dx(2, 2)
             quant_tok(LAST, 0)
             spread_h(0, 1, "v")
             quant_h(0, 0)

@@ -72,7 +72,7 @@ def tile_scm_mlp_pa_v_kernel(tc, h_in, w, masks, mu, sigma, z, pre, grad_out, ou
         w_t = {}
         masked, tok_by4, feat_by4, h_by4, w_by4 = {}, {}, {}, {}, {}
         feat_codes, feat_scales = {}, {}
-        turn_bank, dx_bank, dw_bank = {}, {}, {}
+        turn_bank, dx_bank, dw_bank, dw_done = {}, {}, {}, {}
 
         def move(engine, out, in_):
             if engine == "s":
@@ -203,8 +203,10 @@ def tile_scm_mlp_pa_v_kernel(tc, h_in, w, masks, mu, sigma, z, pre, grad_out, ou
             nc.sync.dma_start(out=dx_v[:, g : g + count, :], in_=rows)
 
         def dw(f, t, n, g):
-            if g == 0:
+            done = dw_done.setdefault((f, t, n), [])
+            if not done:
                 dw_bank[f, t, n] = bank(PACK * n + t)
+            done.append(g)
             cols = span(8 * g + 4 * f + t, P)
             nc.tensor.matmul_mx(
                 out=dw_bank[f, t, n][:],
@@ -212,8 +214,8 @@ def tile_scm_mlp_pa_v_kernel(tc, h_in, w, masks, mu, sigma, z, pre, grad_out, ou
                 lhsT_scale=z_tok_scales[:, cols],
                 rhs=h_codes[:, span(2 * g + n, HALF)].bitcast(E4M3),
                 rhs_scale=h_scales[:, span(2 * g + n, HALF)],
-                start=(g == 0),
-                stop=(g == LAST),
+                start=(len(done) == 1),
+                stop=(len(done) == GROUPS),
             )
 
         def dw_out(f, t, halves=range(2)):
@@ -291,10 +293,10 @@ def tile_scm_mlp_pa_v_kernel(tc, h_in, w, masks, mu, sigma, z, pre, grad_out, ou
             quant_w(0, 0)
             dx_first(0, 0)
             mask_w(1, 1)
-            spread_w(1, 1)
             load_h(2, 2)
             quant_w(0, 1)
             dx_first(1, 0)
+            spread_w(1, 1, "v")
             quant_w(1, 0)
             dx_first(0, 1)
             for s in range(2, 2 * GROUPS):
@@ -348,21 +350,19 @@ def tile_scm_mlp_pa_v_kernel(tc, h_in, w, masks, mu, sigma, z, pre, grad_out, ou
             spread_dz(2, 1, "s")
             quant_tok(1, 1)
             dw_out(0, 0)
-            store_dw(0, span(0, INS))
             dw_tile(1, 0, [0, 1])
             spread_dz(3, 1, "s")
             dw_out(0, 1)
-            store_dw(0, span(1, INS))
+            store_dw(0, span(0, 2 * INS))
             dw_tile(1, 1, [0, 1])
             quant_tok(2, 1)
             dw_out(0, 2)
-            store_dw(0, span(2, INS))
             dw_tile(1, 0, [2])
             dw_tile(1, 1, [2])
             dw_tile(1, 2, [0, 1])
             quant_tok(3, 1)
             dw_out(0, 3)
-            store_dw(0, span(3, INS))
+            store_dw(0, span(1, 2 * INS))
             for t in range(LAST):
                 dw_tile(1, t, [LAST] if t < 2 else [2, LAST])
                 dw_out(1, t)

@@ -139,25 +139,34 @@ def tile_scm_mlp_pa_v_kernel(tc, h_in, w, masks, mu, sigma, z, pre, grad_out, ou
             nc.vector.quantize_mx(out=codes.bitcast(E5M2), scales=scales, in_=feat_by4[g, a][:])
             feat_codes[g, a], feat_scales[g, a] = codes, scales
 
-        def spread_dz(g, f, engine="v"):
-            new = pool.tile([P, PACK * HALF], BF16, tag="by4", bufs=6, align_bytes=64, name="tok_tile")
+        def spread_dz(g, f, engine="v", places=range(PACK)):
+            new = pool.tile([P, len(places) * HALF], BF16, tag="by4", bufs=6, align_bytes=64, name="tok_tile")
             src = dz_t[g].rearrange("p (j w) -> p j w", j=PACK)[:, :, span(f, HALF)]
             move(
                 engine,
-                new[:].rearrange("p (t c r j) -> p c j r t", t=PACK, r=2, j=PACK),
-                src.rearrange("p j (c r t) -> p c j r t", r=2, t=PACK),
+                new[:].rearrange("p (t c r j) -> p c j r t", t=len(places), r=2, j=PACK),
+                src.rearrange("p j (c r t) -> p c j r t", r=2, t=PACK)[:, :, :, :, places.start : places.stop],
             )
-            tok_by4[g, f] = new
+            tok_by4[g, f, places.start] = new
 
-        def quant_tok(g, f):
-            cols = span(2 * g + f, HALF)
+        def quant_tok(g, f, places=range(PACK)):
+            first = (2 * g + f) * HALF
+            cols = slice(first + places.start * P, first + places.stop * P)
             nc.vector.quantize_mx(
-                out=z_tok_codes[:, cols].bitcast(E5M2), scales=z_tok_scales[:, cols], in_=tok_by4[g, f][:]
+                out=z_tok_codes[:, cols].bitcast(E5M2),
+                scales=z_tok_scales[:, cols],
+                in_=tok_by4[g, f, places.start][:],
             )
 
-        def by4(engine, src):
+        def by4(engines, src):
             new = pool.tile([P, PACK * HALF], BF16, tag="by4", bufs=6, align_bytes=64, name="by4_tile")
-            move(engine, new[:].rearrange("p (c i t) -> p c t i", i=4, t=PACK), src.rearrange("p t (c i) -> p c t i", i=4))
+            width = HALF // len(engines)
+            for k, engine in enumerate(engines):
+                move(
+                    engine,
+                    new[:, span(k, PACK * width)].rearrange("p (c i t) -> p c t i", i=4, t=PACK),
+                    src[:, :, span(k, width)].rearrange("p t (c i) -> p c t i", i=4),
+                )
             return new
 
         def spread_h(g, n, engine="s"):
@@ -205,7 +214,7 @@ def tile_scm_mlp_pa_v_kernel(tc, h_in, w, masks, mu, sigma, z, pre, grad_out, ou
         def dw(f, t, n, g):
             done = dw_done.setdefault((f, t, n), [])
             if not done:
-                dw_bank[f, t, n] = bank(PACK * n + t)
+                dw_bank[f, t, n] = next_bank()
             done.append(g)
             cols = span(8 * g + 4 * f + t, P)
             nc.tensor.matmul_mx(
@@ -243,34 +252,25 @@ def tile_scm_mlp_pa_v_kernel(tc, h_in, w, masks, mu, sigma, z, pre, grad_out, ou
                 if f == 1:
                     dx_out(0, j, n)
 
-        def load_group(g):
+        def load_group(g, pieces=2):
             load_grad(g)
-            load_pre(g, 0)
-            load_pre(g, 1)
+            for a in range(pieces):
+                load_pre(g, a, ROWS // pieces)
 
-        def dw_first(g, n):
-            quant_h(g, n)
-            for t in range(PACK):
-                dw(0, t, n, g)
+        def dw_quarter(f, n, g, places=range(PACK)):
+            for t in places:
+                dw(f, t, n, g)
 
-        def dw_quarter(f, n, groups):
-            for g in groups:
-                for t in range(PACK):
-                    dw(f, t, n, g)
-
-        def dw_tile(f, t, groups):
-            for g in groups:
-                for n in range(2):
-                    dw(f, t, n, g)
+        def dw_quarter_out(f, n, places=range(PACK)):
+            for t in places:
+                dw_out(f, t, [n])
 
         with tc.manual_schedule():
-            for a in range(2):
-                load_grad(0, span(a, PAIR))
-                load_pre(0, a)
+            load_group(0)
             for f in range(2):
                 load_w(f)
             for g in range(1, GROUPS):
-                load_group(g)
+                load_group(g, 2)
             load_h(0, 2)
             gate(0, 0)
             turn(0, 0)
@@ -311,64 +311,77 @@ def tile_scm_mlp_pa_v_kernel(tc, h_in, w, masks, mu, sigma, z, pre, grad_out, ou
                     dx_first(1, 1)
                 else:
                     quant_feat(*before)
-                if a == 1:
+                if a == 1 and g < LAST:
                     spread_dz(g, 0)
-                elif g > 1:
+                elif a == 0 and g > 1:
                     quant_tok(g - 1, 0)
                 if s > 2:
                     dx_pair(*before)
+            low, high = range(0, 2), range(2, PACK)
             spread_h(0, 0, "v")
+            spread_h(1, 0, "v")
             quant_feat(LAST, 1)
             dx_pair(LAST, 1)
             store_dx(0, 2)
             store_dx(2, 2)
-            quant_tok(LAST, 0)
-            spread_h(0, 1, "v")
             quant_h(0, 0)
-            spread_h(1, 0, "v")
-            quant_h(0, 1)
-            spread_h(1, 1, "v")
             quant_h(1, 0)
-            spread_h(2, 1, "s")
+            dw_quarter(0, 0, 0)
+            dw_quarter(0, 0, 1)
             spread_h(2, 0, "v")
-            quant_h(1, 1)
-            spread_h(3, 1, "s")
-            quant_h(2, 0)
+            spread_h(0, 1, "s")
             spread_h(3, 0, "v")
-            quant_h(2, 1)
-            spread_dz(1, 1, "s")
+            quant_h(2, 0)
+            dw_quarter(0, 0, 2)
+            spread_dz(LAST, 0)
             quant_h(3, 0)
+            quant_h(0, 1)
+            dw_quarter(0, 1, 0)
+            spread_h(1, 1, "s")
+            quant_tok(LAST, 0)
+            dw_quarter(0, 0, 3)
+            spread_h(3, 1, "v")
+            spread_h(2, 1, "s")
+            quant_h(1, 1)
+            dw_quarter(0, 1, 1)
             quant_h(3, 1)
-            for t in range(PACK):
-                dw_tile(0, t, [0])
-            for g in range(1, LAST):
+            dw_quarter(0, 1, 3)
+            dw_quarter_out(0, 0, low)
+            dw_quarter(1, 0, 0, low)
+            for g in range(1, GROUPS):
+                spread_dz(g, 1, "s", low)
+            quant_h(2, 1)
+            dw_quarter(0, 1, 2)
+            dw_quarter_out(0, 0, high)
+            dw_quarter(1, 1, 0, low)
+            quant_tok(1, 1, low)
+            spread_dz(1, 1, "s", high)
+            for n in range(2):
+                dw_quarter(1, n, 1, low)
+            dw_quarter_out(0, 1, low)
+            quant_tok(2, 1, low)
+            spread_dz(2, 1, "s", high)
+            for n in range(2):
+                dw_quarter(1, n, 2, low)
+            dw_quarter_out(0, 1, high)
+            store_dw(0, span(0, ROWS))
+            quant_tok(3, 1, low)
+            spread_dz(3, 1, "s", high)
+            for t in low:
                 for n in range(2):
-                    for t in range(PACK):
-                        dw(0, t, n, g)
-            for t in range(PACK):
-                dw_tile(0, t, [LAST])
-            spread_dz(2, 1, "s")
-            quant_tok(1, 1)
-            dw_out(0, 0)
-            dw_tile(1, 0, [0, 1])
-            spread_dz(3, 1, "s")
-            dw_out(0, 1)
-            store_dw(0, span(0, 2 * INS))
-            dw_tile(1, 1, [0, 1])
-            quant_tok(2, 1)
-            dw_out(0, 2)
-            dw_tile(1, 0, [2])
-            dw_tile(1, 1, [2])
-            dw_tile(1, 2, [0, 1])
-            quant_tok(3, 1)
-            dw_out(0, 3)
-            store_dw(0, span(1, 2 * INS))
-            for t in range(LAST):
-                dw_tile(1, t, [LAST] if t < 2 else [2, LAST])
+                    dw(1, t, n, 3)
+            quant_tok(1, 1, high)
+            for g in range(2):
+                for n in range(2):
+                    dw_quarter(1, n, g, high)
+            dw_out(1, 0)
+            quant_tok(2, 1, high)
+            dw_out(1, 1)
+            quant_tok(3, 1, high)
+            store_dw(1, span(0, 2 * INS))
+            for t in high:
+                for n in range(2):
+                    for g in range(2, GROUPS):
+                        dw(1, t, n, g)
                 dw_out(1, t)
                 store_dw(1, span(t, INS))
-            for n in range(2):
-                for g in range(GROUPS):
-                    dw(1, LAST, n, g)
-                dw_out(1, LAST, [n])
-            store_dw(1, span(LAST, INS))

@@ -58,13 +58,13 @@ def tile_scm_mlp_pa_v_kernel(tc, h_in, w, masks, mu, sigma, z, pre, grad_out, ou
         h_scales = placed(keep, "h_scales", GROUPS * INS, U8, 128)
         w_codes = placed(keep, "w_codes", 2 * INS, U32, 0)
         w_scales = placed(keep, "w_scales", 2 * INS, U8, 128)
-        mask = keep.tile([P, 2 * PACK * INS], BF16, align_bytes=64, name="mask")
+        mask = keep.tile([P, 2 * PACK * INS], BF16, align_bytes=256, name="mask")
 
-        pre_all = keep.tile([P, GROUPS * ROWS], F32, name="pre_all")
-        dz_all = keep.tile([P, GROUPS * ROWS], BF16, align_bytes=64, name="dz_all")
+        pre_all = keep.tile([P, GROUPS * ROWS], F32, align_bytes=256, name="pre_all")
+        dz_all = keep.tile([P, GROUPS * ROWS], BF16, align_bytes=256, name="dz_all")
         pre_t = [pre_all[:, span(g, ROWS)] for g in range(GROUPS)]
         dz_t = [dz_all[:, span(g, ROWS)] for g in range(GROUPS)]
-        h_all = keep.tile([P, GROUPS * ROWS], BF16, name="h_all")
+        h_all = keep.tile([P, GROUPS * ROWS], BF16, align_bytes=256, name="h_all")
         w_all = h_all[:, 2 * ROWS : 4 * ROWS]
         h_t = [h_all[:, span(g, ROWS)] for g in range(GROUPS)]
         dw_t = [h_all[:].bitcast(F32)[:, span(f, ROWS)] for f in range(2)]

@@ -288,15 +288,15 @@ def tile_scm_mlp_pa_v_kernel(tc, h_in, w, masks, mu, sigma, z, pre, grad_out, ou
             quant_tok(0, 0)
             quant_feat(0, 1)
             quant_tok(0, 1)
-            mask_w(1, 0)
-            spread_w(1, 0)
             quant_w(0, 0)
             dx_first(0, 0)
+            mask_w(1, 0)
             mask_w(1, 1)
             load_h(2, 2)
+            spread_w(1, 0, "sv")
+            spread_w(1, 1, "s")
             quant_w(0, 1)
             dx_first(1, 0)
-            spread_w(1, 1, "v")
             quant_w(1, 0)
             dx_first(0, 1)
             for s in range(2, 2 * GROUPS):

@@ -164,8 +164,8 @@ def tile_scm_mlp_pa_v_kernel(tc, h_in, w, masks, mu, sigma, z, pre, grad_out, ou
             for k, engine in enumerate(engines):
                 move(
                     engine,
-                    new[:, span(k, PACK * width)].rearrange("p (c i t) -> p c t i", i=4, t=PACK),
-                    src[:, :, span(k, width)].rearrange("p t (c i) -> p c t i", i=4),
+                    new[:, span(k, PACK * width)].rearrange("p (c i t) -> p c t i", i=8, t=PACK),
+                    src[:, :, span(k, width)].rearrange("p t (c i) -> p c t i", i=8),
                 )
             return new
 

@@ -69,7 +69,7 @@ def tile_scm_mlp_pa_v_kernel(tc, h_in, w, masks, mu, sigma, z, pre, grad_out, ou
         h_t = [h_all[:, span(g, ROWS)] for g in range(GROUPS)]
         dw_t = [h_all[:].bitcast(F32)[:, span(f, ROWS)] for f in range(2)]
 
-        w_t = {}
+        w_t, opened = {}, {}
         masked, tok_by4, feat_by4, h_by4, w_by4 = {}, {}, {}, {}, {}
         feat_codes, feat_scales = {}, {}
         turn_bank, dx_bank, dw_bank, dw_done = {}, {}, {}, {}
@@ -109,6 +109,17 @@ def tile_scm_mlp_pa_v_kernel(tc, h_in, w, masks, mu, sigma, z, pre, grad_out, ou
             nc.vector.scalar_tensor_tensor(
                 out=rows, in0=pre_t[g][:, span(a, width)], scalar=0.0, in1=rows, op0=IS_GT, op1=MULT
             )
+
+        def open_mask(g, a):
+            new = pool.tile([P, PAIR], BF16, tag="by4", bufs=6, align_bytes=64, name="open_tile")
+            nc.vector.tensor_scalar(
+                out=new[:], in0=pre_t[g][:, span(a, PAIR)], scalar1=0.0, scalar2=None, op0=IS_GT
+            )
+            opened[g, a] = new
+
+        def product(g, a):
+            rows = dz_t[g][:, span(a, PAIR)]
+            nc.vector.tensor_tensor(out=rows, in0=rows, in1=opened[g, a][:], op=MULT)
 
         def turn(g, a):
             words = dz_t[g].bitcast(F32)
@@ -239,12 +250,15 @@ def tile_scm_mlp_pa_v_kernel(tc, h_in, w, masks, mu, sigma, z, pre, grad_out, ou
         def store_dw(f, cols):
             nc.sync.dma_start(out=dw_v[f, :, cols], in_=dw_t[f][:, cols])
 
+        def dx_row(g, j):
+            for n in range(2):
+                for f in range(2):
+                    dx(g, j, n, f)
+                dx_out(g, j, n)
+
         def dx_pair(g, a):
             for j in (2 * a, 2 * a + 1):
-                for n in range(2):
-                    for f in range(2):
-                        dx(g, j, n, f)
-                    dx_out(g, j, n)
+                dx_row(g, j)
 
         def dx_first(n, f):
             for j in range(PACK):
@@ -269,8 +283,10 @@ def tile_scm_mlp_pa_v_kernel(tc, h_in, w, masks, mu, sigma, z, pre, grad_out, ou
             load_group(0)
             for f in range(2):
                 load_w(f)
-            for g in range(1, GROUPS):
-                load_group(g, 2)
+            load_group(1)
+            for g in range(2, GROUPS):
+                load_pre(g, 0, ROWS)
+                load_grad(g)
             load_h(0, 2)
             gate(0, 0)
             turn(0, 0)
@@ -299,26 +315,37 @@ def tile_scm_mlp_pa_v_kernel(tc, h_in, w, masks, mu, sigma, z, pre, grad_out, ou
             dx_first(1, 0)
             quant_w(1, 0)
             dx_first(0, 1)
-            for s in range(2, 2 * GROUPS):
-                g, a = divmod(s, 2)
-                before = divmod(s - 1, 2)
-                gate(g, a)
-                if s == 2:
-                    quant_w(1, 1)
-                turn(g, a)
-                turn_out(g, a)
-                if s == 2:
-                    dx_first(1, 1)
-                else:
-                    quant_feat(*before)
-                if a == 1 and g < LAST:
+            gate(1, 0)
+            quant_w(1, 1)
+            turn(1, 0)
+            turn_out(1, 0)
+            dx_first(1, 1)
+            gate(1, 1)
+            turn(1, 1)
+            turn_out(1, 1)
+            quant_feat(1, 0)
+            spread_dz(1, 0)
+            dx_pair(1, 0)
+            for g in range(2, GROUPS):
+                open_mask(g, 0)
+                quant_feat(g - 1, 1)
+                dx_row(g - 1, 2)
+                product(g, 0)
+                turn(g, 0)
+                turn_out(g, 0)
+                dx_row(g - 1, 3)
+                open_mask(g, 1)
+                quant_tok(g - 1, 0)
+                product(g, 1)
+                turn(g, 1)
+                turn_out(g, 1)
+                quant_feat(g, 0)
+                if g < LAST:
                     spread_dz(g, 0)
-                elif a == 0 and g > 1:
-                    quant_tok(g - 1, 0)
-                if s > 2:
-                    dx_pair(*before)
+                else:
+                    spread_h(0, 0, "v")
+                dx_pair(g, 0)
             low, high = range(0, 2), range(2, PACK)
-            spread_h(0, 0, "v")
             spread_h(1, 0, "v")
             quant_feat(LAST, 1)
             dx_pair(LAST, 1)

@@ -283,10 +283,10 @@ def tile_scm_mlp_pa_v_kernel(tc, h_in, w, masks, mu, sigma, z, pre, grad_out, ou
             load_group(0)
             for f in range(2):
                 load_w(f)
-            load_group(1)
-            for g in range(2, GROUPS):
-                load_pre(g, 0, ROWS)
-                load_grad(g)
+            for g in range(1, LAST):
+                load_group(g)
+            load_pre(LAST, 0, ROWS)
+            load_grad(LAST)
             load_h(0, 2)
             gate(0, 0)
             turn(0, 0)
@@ -315,36 +315,39 @@ def tile_scm_mlp_pa_v_kernel(tc, h_in, w, masks, mu, sigma, z, pre, grad_out, ou
             dx_first(1, 0)
             quant_w(1, 0)
             dx_first(0, 1)
-            gate(1, 0)
-            quant_w(1, 1)
-            turn(1, 0)
-            turn_out(1, 0)
-            dx_first(1, 1)
-            gate(1, 1)
-            turn(1, 1)
-            turn_out(1, 1)
-            quant_feat(1, 0)
-            spread_dz(1, 0)
-            dx_pair(1, 0)
-            for g in range(2, GROUPS):
-                open_mask(g, 0)
-                quant_feat(g - 1, 1)
-                dx_row(g - 1, 2)
-                product(g, 0)
-                turn(g, 0)
-                turn_out(g, 0)
-                dx_row(g - 1, 3)
-                open_mask(g, 1)
-                quant_tok(g - 1, 0)
-                product(g, 1)
-                turn(g, 1)
-                turn_out(g, 1)
-                quant_feat(g, 0)
-                if g < LAST:
-                    spread_dz(g, 0)
+            for s in range(2, 2 * LAST):
+                g, a = divmod(s, 2)
+                before = divmod(s - 1, 2)
+                gate(g, a)
+                if s == 2:
+                    quant_w(1, 1)
+                turn(g, a)
+                turn_out(g, a)
+                if s == 2:
+                    dx_first(1, 1)
                 else:
-                    spread_h(0, 0, "v")
-                dx_pair(g, 0)
+                    quant_feat(*before)
+                if a == 1:
+                    spread_dz(g, 0)
+                elif g > 1:
+                    quant_tok(g - 1, 0)
+                if s > 2:
+                    dx_pair(*before)
+            open_mask(LAST, 0)
+            quant_feat(LAST - 1, 1)
+            dx_row(LAST - 1, 2)
+            product(LAST, 0)
+            turn(LAST, 0)
+            turn_out(LAST, 0)
+            dx_row(LAST - 1, 3)
+            open_mask(LAST, 1)
+            quant_tok(LAST - 1, 0)
+            product(LAST, 1)
+            turn(LAST, 1)
+            turn_out(LAST, 1)
+            quant_feat(LAST, 0)
+            spread_h(0, 0, "v")
+            dx_pair(LAST, 0)
             low, high = range(0, 2), range(2, PACK)
             spread_h(1, 0, "v")
             quant_feat(LAST, 1)

@@ -389,23 +389,24 @@ def tile_scm_mlp_pa_v_kernel(tc, h_in, w, masks, mu, sigma, z, pre, grad_out, ou
             for n in range(2):
                 dw_quarter(1, n, 1, low)
             dw_quarter_out(0, 1, low)
-            quant_tok(2, 1, low)
-            spread_dz(2, 1, "s", high)
-            for n in range(2):
-                dw_quarter(1, n, 2, low)
+            dw_quarter(1, 0, 0, high)
             dw_quarter_out(0, 1, high)
             store_dw(0, span(0, ROWS))
+            quant_tok(2, 1, low)
+            spread_dz(2, 1, "s", high)
             quant_tok(3, 1, low)
             spread_dz(3, 1, "s", high)
+            for n in range(2):
+                dw_quarter(1, n, 2, low)
             for t in low:
                 for n in range(2):
                     dw(1, t, n, 3)
             quant_tok(1, 1, high)
-            for g in range(2):
-                for n in range(2):
-                    dw_quarter(1, n, g, high)
-            dw_out(1, 0)
+            dw_quarter(1, 1, 0, high)
+            for n in range(2):
+                dw_quarter(1, n, 1, high)
             quant_tok(2, 1, high)
+            dw_out(1, 0)
             dw_out(1, 1)
             quant_tok(3, 1, high)
             store_dw(1, span(0, 2 * INS))

@@ -353,7 +353,8 @@ def tile_scm_mlp_pa_v_kernel(tc, h_in, w, masks, mu, sigma, z, pre, grad_out, ou
             quant_feat(LAST, 1)
             dx_pair(LAST, 1)
             store_dx(0, 2)
-            store_dx(2, 2)
+            store_dx(2, 1)
+            store_dx(3, 1)
             quant_h(0, 0)
             quant_h(1, 0)
             dw_quarter(0, 0, 0)

from contextlib import ExitStack

import concourse.mybir as mybir
from concourse.masks import make_identity

TOKENS, FEATS, INS = 2048, 1024, 1024
FLOPS = 2 * (2 * TOKENS * FEATS * INS)
BYTES = 2 * (TOKENS * INS + 2 * FEATS * INS + TOKENS * FEATS) + 4 * (TOKENS * FEATS + TOKENS * INS + FEATS * INS)

F32 = mybir.dt.float32
BF16 = mybir.dt.bfloat16
U32 = mybir.dt.uint32
U8 = mybir.dt.uint8
E4M3 = mybir.dt.float8_e4m3fn_x4
E5M2 = mybir.dt.float8_e5m2_x4
MULT = mybir.AluOpType.mult
IS_GT = mybir.AluOpType.is_gt

P = 128
PACK = 4
HALF = P * PACK
GROUPS = TOKENS // HALF
LAST = GROUPS - 1
BANKS = 8
PAIR = 2 * FEATS
ROWS = PACK * INS


def tile_scm_mlp_pa_v_kernel(tc, h_in, w, masks, mu, sigma, z, pre, grad_out, out_0, out_1):
    nc = tc.nc
    pre_v = pre.rearrange("(g p j) w -> p g (j w)", p=P, j=PACK)
    grad_v = grad_out.rearrange("(g p j) w -> p g (j w)", p=P, j=PACK)
    h_v = h_in.rearrange("(g p j) i -> p g (j i)", p=P, j=PACK)
    w_v = w[0, :, :].rearrange("(f q t) i -> f q (t i)", q=P, t=PACK)
    mask_v = masks[0, :, :].rearrange("(f q t) i -> f q (t i)", q=P, t=PACK)
    dx_v = out_0.rearrange("(g p j) i -> p g (j i)", p=P, j=PACK)
    dw_v = out_1[0, :, :].rearrange("(f q t) i -> f q (t i)", q=P, t=PACK)

    def span(k, width):
        return slice(k * width, (k + 1) * width)

    with ExitStack() as ctx:
        keep = ctx.enter_context(tc.tile_pool(name="keep", bufs=1))
        pool = ctx.enter_context(tc.tile_pool(name="pool", bufs=2))
        psum = ctx.enter_context(tc.psum_pool(name="psum", bufs=1))

        ident = keep.tile([P, P], F32, name="ident")
        make_identity(nc, ident[:])

        def placed(where, tag, words, dtype, skip, bufs=1):
            pad = skip if dtype is U8 else skip // 4
            new = where.tile([P, words + pad], dtype, tag=tag, bufs=bufs, align_bytes=256, name="placed_tile")
            return new[:, pad : pad + words]

        z_tok_codes = placed(keep, "z_tok_codes", GROUPS * FEATS, U32, 64)
        z_tok_scales = placed(keep, "z_tok_scales", GROUPS * FEATS, U8, 192)
        h_codes = placed(keep, "h_codes", GROUPS * INS, U32, 0)
        h_scales = placed(keep, "h_scales", GROUPS * INS, U8, 128)
        w_codes = placed(keep, "w_codes", 2 * INS, U32, 0)
        w_scales = placed(keep, "w_scales", 2 * INS, U8, 128)
        mask = keep.tile([P, 2 * PACK * INS], BF16, align_bytes=256, name="mask")

        pre_all = keep.tile([P, GROUPS * ROWS], F32, align_bytes=256, name="pre_all")
        dz_all = keep.tile([P, GROUPS * ROWS], BF16, align_bytes=256, name="dz_all")
        pre_t = [pre_all[:, span(g, ROWS)] for g in range(GROUPS)]
        dz_t = [dz_all[:, span(g, ROWS)] for g in range(GROUPS)]
        h_all = keep.tile([P, GROUPS * ROWS], BF16, align_bytes=256, name="h_all")
        w_all = h_all[:, 2 * ROWS : 4 * ROWS]
        h_t = [h_all[:, span(g, ROWS)] for g in range(GROUPS)]
        dw_t = [h_all[:].bitcast(F32)[:, span(f, ROWS)] for f in range(2)]

        w_t, opened = {}, {}
        masked, tok_by4, feat_by4, h_by4, w_by4 = {}, {}, {}, {}, {}
        feat_codes, feat_scales = {}, {}
        turn_bank, dx_bank, dw_bank, dw_done = {}, {}, {}, {}

        def move(engine, out, in_):
            if engine == "s":
                nc.scalar.copy(out=out, in_=in_)
            else:
                nc.vector.tensor_copy(out=out, in_=in_)

        def bank(b):
            return psum.tile([P, HALF], F32, tag="bank%d" % b, name="bank_tile")

        taken = []

        def next_bank():
            taken.append(len(taken) % BANKS)
            return bank(taken[-1])

        def load_pre(g, a, width=PAIR):
            nc.sync.dma_start(out=pre_t[g][:, span(a, width)], in_=pre_v[:, g, span(a, width)])

        def load_grad(g, cols=slice(0, ROWS)):
            nc.sync.dma_start(out=dz_t[g][:, cols], in_=grad_v[:, g, cols])

        def load_h(g, count):
            rows = h_all[:, g * ROWS : (g + count) * ROWS].rearrange("p (g c) -> p g c", g=count)
            nc.sync.dma_start(out=rows, in_=h_v[:, g : g + count, :])

        def load_w(f):
            nc.sync.dma_start(out=w_all[:, span(f, ROWS)], in_=w_v[f, :, :])
            nc.sync.dma_start(out=mask[:, span(f, ROWS)], in_=mask_v[f, :, :])
            w_t[f] = w_all[:, span(f, ROWS)]

        def gate(g, a, width=PAIR):
            rows = dz_t[g][:, span(a, width)]
            nc.vector.scalar_tensor_tensor(
                out=rows, in0=pre_t[g][:, span(a, width)], scalar=0.0, in1=rows, op0=IS_GT, op1=MULT
            )

        def open_mask(g, a):
            new = pool.tile([P, PAIR], BF16, tag="by4", bufs=6, align_bytes=64, name="open_tile")
            nc.vector.tensor_scalar(
                out=new[:], in0=pre_t[g][:, span(a, PAIR)], scalar1=0.0, scalar2=None, op0=IS_GT
            )
            opened[g, a] = new

        def product(g, a):
            rows = dz_t[g][:, span(a, PAIR)]
            nc.vector.tensor_tensor(out=rows, in0=rows, in1=opened[g, a][:], op=MULT)

        def turn(g, a):
            words = dz_t[g].bitcast(F32)
            for f in range(2):
                new = next_bank()
                for k in range(2):
                    for u in range(2):
                        first = (2 * a + k) * (FEATS // 2) + f * (HALF // 2) + u
                        nc.tensor.transpose(
                            new[:, span(2 * k + u, P)], words[:, first : first + HALF // 2 - 1 : 2], ident[:]
                        )
                turn_bank[g, a, f] = new

        def turn_out(g, a, engines="ss"):
            new = pool.tile([P, PAIR], BF16, tag="feat_by4", align_bytes=64, name="feat_tile")
            words = new[:].bitcast(F32)
            for f in range(2):
                move(
                    engines[f],
                    words[:, span(f, HALF)].rearrange("q (k p u) -> q k p u", k=2, u=2),
                    turn_bank[g, a, f][:].rearrange("q (k u p) -> q k p u", k=2, u=2),
                )
            feat_by4[g, a] = new

        def quant_feat(g, a):
            codes = placed(pool, "feat_codes", HALF, U32, 64, bufs=3)
            scales = placed(pool, "feat_scales", HALF, U8, 192, bufs=3)
            nc.vector.quantize_mx(out=codes.bitcast(E5M2), scales=scales, in_=feat_by4[g, a][:])
            feat_codes[g, a], feat_scales[g, a] = codes, scales

        def spread_dz(g, f, engine="v", places=range(PACK)):
            new = pool.tile([P, len(places) * HALF], BF16, tag="by4", bufs=6, align_bytes=64, name="tok_tile")
            src = dz_t[g].rearrange("p (j w) -> p j w", j=PACK)[:, :, span(f, HALF)]
            move(
                engine,
                new[:].rearrange("p (t c r j) -> p c j r t", t=len(places), r=2, j=PACK),
                src.rearrange("p j (c r t) -> p c j r t", r=2, t=PACK)[:, :, :, :, places.start : places.stop],
            )
            tok_by4[g, f, places.start] = new

        def quant_tok(g, f, places=range(PACK)):
            first = (2 * g + f) * HALF
            cols = slice(first + places.start * P, first + places.stop * P)
            nc.vector.quantize_mx(
                out=z_tok_codes[:, cols].bitcast(E5M2),
                scales=z_tok_scales[:, cols],
                in_=tok_by4[g, f, places.start][:],
            )

        def by4(engines, src):
            new = pool.tile([P, PACK * HALF], BF16, tag="by4", bufs=6, align_bytes=64, name="by4_tile")
            width = HALF // len(engines)
            for k, engine in enumerate(engines):
                move(
                    engine,
                    new[:, span(k, PACK * width)].rearrange("p (c i t) -> p c t i", i=8, t=PACK),
                    src[:, :, span(k, width)].rearrange("p t (c i) -> p c t i", i=8),
                )
            return new

        def spread_h(g, n, engine="s"):
            h_by4[g, n] = by4(engine, h_t[g].rearrange("p (j i) -> p j i", j=PACK)[:, :, span(n, HALF)])

        def quant_h(g, n):
            cols = span(2 * g + n, HALF)
            nc.vector.quantize_mx(out=h_codes[:, cols].bitcast(E4M3), scales=h_scales[:, cols], in_=h_by4[g, n][:])

        def mask_w(f, n):
            rows = w_t[f].rearrange("q (t i) -> q t i", t=PACK)[:, :, span(n, HALF)]
            keeps = mask[:, span(f, ROWS)].rearrange("q (t i) -> q t i", t=PACK)[:, :, span(n, HALF)]
            new = pool.tile([P, PACK * HALF], BF16, tag="by4", bufs=6, align_bytes=64, name="masked_tile")
            nc.vector.tensor_tensor(out=new[:].rearrange("q (t i) -> q t i", t=PACK), in0=rows, in1=keeps, op=MULT)
            masked[f, n] = new

        def spread_w(f, n, engine="s"):
            w_by4[f, n] = by4(engine, masked[f, n][:].rearrange("q (t i) -> q t i", t=PACK))

        def quant_w(f, n):
            cols = span(2 * f + n, HALF)
            nc.vector.quantize_mx(out=w_codes[:, cols].bitcast(E4M3), scales=w_scales[:, cols], in_=w_by4[f, n][:])

        def dx(g, j, n, f):
            a, k = divmod(j, 2)
            if f == 0:
                dx_bank[g, j, n] = next_bank()
            nc.tensor.matmul_mx(
                out=dx_bank[g, j, n][:],
                lhsT=feat_codes[g, a][:, span(2 * f + k, P)].bitcast(E5M2),
                lhsT_scale=feat_scales[g, a][:, span(2 * f + k, P)],
                rhs=w_codes[:, span(2 * f + n, HALF)].bitcast(E4M3),
                rhs_scale=w_scales[:, span(2 * f + n, HALF)],
                start=(f == 0),
                stop=(f == 1),
            )

        def dx_out(g, j, n):
            nc.scalar.copy(out=pre_t[g][:, span(2 * j + n, HALF)], in_=dx_bank[g, j, n][:])

        def store_dx(g, count):
            rows = pre_all[:, g * ROWS : (g + count) * ROWS].rearrange("p (g c) -> p g c", g=count)
            nc.sync.dma_start(out=dx_v[:, g : g + count, :], in_=rows)

        def dw(f, t, n, g):
            done = dw_done.setdefault((f, t, n), [])
            if not done:
                dw_bank[f, t, n] = next_bank()
            done.append(g)
            cols = span(8 * g + 4 * f + t, P)
            nc.tensor.matmul_mx(
                out=dw_bank[f, t, n][:],
                lhsT=z_tok_codes[:, cols].bitcast(E5M2),
                lhsT_scale=z_tok_scales[:, cols],
                rhs=h_codes[:, span(2 * g + n, HALF)].bitcast(E4M3),
                rhs_scale=h_scales[:, span(2 * g + n, HALF)],
                start=(len(done) == 1),
                stop=(len(done) == GROUPS),
            )

        def dw_out(f, t, halves=range(2)):
            for n in halves:
                nc.vector.tensor_tensor(
                    out=dw_t[f][:, span(2 * t + n, HALF)],
                    in0=dw_bank[f, t, n][:],
                    in1=mask[:, span(8 * f + 2 * t + n, HALF)],
                    op=MULT,
                )

        def store_dw(f, cols):
            nc.sync.dma_start(out=dw_v[f, :, cols], in_=dw_t[f][:, cols])

        def dx_row(g, j):
            for n in range(2):
                for f in range(2):
                    dx(g, j, n, f)
                dx_out(g, j, n)

        def dx_pair(g, a):
            for j in (2 * a, 2 * a + 1):
                dx_row(g, j)

        def dx_first(n, f):
            for j in range(PACK):
                dx(0, j, n, f)
                if f == 1:
                    dx_out(0, j, n)

        def load_group(g, pieces=2):
            load_grad(g)
            for a in range(pieces):
                load_pre(g, a, ROWS // pieces)

        def dw_quarter(f, n, g, places=range(PACK)):
            for t in places:
                dw(f, t, n, g)

        def dw_quarter_out(f, n, places=range(PACK)):
            for t in places:
                dw_out(f, t, [n])

        with tc.manual_schedule():
            load_group(0)
            for f in range(2):
                load_w(f)
            for g in range(1, LAST):
                load_group(g)
            load_pre(LAST, 0, ROWS)
            load_grad(LAST)
            load_h(0, 2)
            gate(0, 0)
            turn(0, 0)
            turn_out(0, 0)
            gate(0, 1)
            turn(0, 1)
            quant_feat(0, 0)
            spread_dz(0, 1, "s")
            spread_dz(0, 0)
            turn_out(0, 1)
            mask_w(0, 0)
            spread_w(0, 0)
            mask_w(0, 1)
            spread_w(0, 1)
            quant_tok(0, 0)
            quant_feat(0, 1)
            quant_tok(0, 1)
            quant_w(0, 0)
            dx_first(0, 0)
            mask_w(1, 0)
            mask_w(1, 1)
            load_h(2, 2)
            spread_w(1, 0, "sv")
            spread_w(1, 1, "s")
            quant_w(0, 1)
            dx_first(1, 0)
            quant_w(1, 0)
            dx_first(0, 1)
            for s in range(2, 2 * LAST):
                g, a = divmod(s, 2)
                before = divmod(s - 1, 2)
                gate(g, a)
                if s == 2:
                    quant_w(1, 1)
                turn(g, a)
                turn_out(g, a)
                if s == 2:
                    dx_first(1, 1)
                else:
                    quant_feat(*before)
                if a == 1:
                    spread_dz(g, 0)
                elif g > 1:
                    quant_tok(g - 1, 0)
                if s > 2:
                    dx_pair(*before)
            open_mask(LAST, 0)
            quant_feat(LAST - 1, 1)
            dx_row(LAST - 1, 2)
            product(LAST, 0)
            turn(LAST, 0)
            turn_out(LAST, 0)
            dx_row(LAST - 1, 3)
            open_mask(LAST, 1)
            quant_tok(LAST - 1, 0)
            product(LAST, 1)
            turn(LAST, 1)
            turn_out(LAST, 1)
            quant_feat(LAST, 0)
            spread_h(0, 0, "v")
            dx_pair(LAST, 0)
            low, high = range(0, 2), range(2, PACK)
            spread_h(1, 0, "v")
            quant_feat(LAST, 1)
            dx_pair(LAST, 1)
            store_dx(0, 2)
            store_dx(2, 1)
            store_dx(3, 1)
            quant_h(0, 0)
            quant_h(1, 0)
            dw_quarter(0, 0, 0)
            dw_quarter(0, 0, 1)
            spread_h(2, 0, "v")
            spread_h(0, 1, "s")
            spread_h(3, 0, "v")
            quant_h(2, 0)
            dw_quarter(0, 0, 2)
            spread_dz(LAST, 0)
            quant_h(3, 0)
            quant_h(0, 1)
            dw_quarter(0, 1, 0)
            spread_h(1, 1, "s")
            quant_tok(LAST, 0)
            dw_quarter(0, 0, 3)
            spread_h(3, 1, "v")
            spread_h(2, 1, "s")
            quant_h(1, 1)
            dw_quarter(0, 1, 1)
            quant_h(3, 1)
            dw_quarter(0, 1, 3)
            dw_quarter_out(0, 0, low)
            dw_quarter(1, 0, 0, low)
            for g in range(1, GROUPS):
                spread_dz(g, 1, "s", low)
            quant_h(2, 1)
            dw_quarter(0, 1, 2)
            dw_quarter_out(0, 0, high)
            dw_quarter(1, 1, 0, low)
            quant_tok(1, 1, low)
            spread_dz(1, 1, "s", high)
            for n in range(2):
                dw_quarter(1, n, 1, low)
            dw_quarter_out(0, 1, low)
            dw_quarter(1, 0, 0, high)
            dw_quarter_out(0, 1, high)
            store_dw(0, span(0, ROWS))
            quant_tok(2, 1, low)
            spread_dz(2, 1, "s", high)
            quant_tok(3, 1, low)
            spread_dz(3, 1, "s", high)
            for n in range(2):
                dw_quarter(1, n, 2, low)
            for t in low:
                for n in range(2):
                    dw(1, t, n, 3)
            quant_tok(1, 1, high)
            dw_quarter(1, 1, 0, high)
            for n in range(2):
                dw_quarter(1, n, 1, high)
            quant_tok(2, 1, high)
            dw_out(1, 0)
            dw_out(1, 1)
            quant_tok(3, 1, high)
            store_dw(1, span(0, 2 * INS))
            for t in high:
                for n in range(2):
                    for g in range(2, GROUPS):
                        dw(1, t, n, g)
                dw_out(1, t)
                store_dw(1, span(t, INS))
